import numpy as np
import ml_dtypes


def mxq(x, axis, fmt="e4m3"):
    dtype, down = {"e4m3": (ml_dtypes.float8_e4m3fn, 7), "e5m2": (ml_dtypes.float8_e5m2, 14)}[fmt]
    v = np.moveaxis(np.asarray(x, np.float32).astype(ml_dtypes.bfloat16).astype(np.float64), axis, -1)
    blocks = v.reshape(v.shape[:-1] + (-1, 32))
    amax = np.abs(blocks).max(-1, keepdims=True)
    byte = np.maximum(np.where(amax > 0, np.frexp(amax)[1] - 1 + 127, 0) - down, 1)
    scale = np.exp2(byte - 127.0)
    codes = (blocks / scale).astype(np.float32).astype(dtype).astype(np.float64)
    return np.moveaxis((codes * scale).reshape(v.shape), -1, axis)


WIDE = False


def mx_kscale(k):
    if not WIDE:
        return np.ones(k)
    levels = np.array([10, -10, 5, -5, 0])
    a = np.random.permutation(np.resize(levels, k // 512 * 4)).reshape(k // 512, 4)
    idx = np.arange(k)
    return np.exp2(a[idx // 512, idx % 128 // 32])


BF16 = ml_dtypes.bfloat16


def bf(x):
    return np.asarray(x, np.float32).astype(BF16)


def f64(x):
    return np.asarray(x).astype(np.float64)


E2M1 = np.array([0.0, 0.5, 1.0, 1.5, 2.0, 3.0, 4.0, 6.0, -0.0, -0.5, -1.0, -1.5, -2.0, -3.0, -4.0, -6.0])


def pack_weight(w, fmt):
    k, n = w.shape
    w = f64(bf(w)).reshape(k // 32, 32, n)
    amax = np.abs(w).max(1)
    if fmt == "e4m3":
        byte = np.frexp(amax)[1] - 1 + 127 - 7
    else:
        mant, ex = np.frexp(amax / 6.0)
        byte = np.where(mant > 0.5, ex, ex - 1) + 127
    byte = np.clip(np.where(amax > 0, byte, 1), 1, 254)
    scaled = (w * np.exp2(127.0 - byte)[:, None, :]).reshape(k, n).astype(np.float32)
    by_word = np.ascontiguousarray(scaled.reshape(k // 512, 128, 4, n).transpose(0, 1, 3, 2))
    if fmt == "e4m3":
        words = by_word.astype(ml_dtypes.float8_e4m3fn).view(np.uint8)
    else:
        c = by_word.astype(ml_dtypes.float4_e2m1fn).view(np.uint8) & 0xF
        words = c[..., 0::2] | (c[..., 1::2] << 4)
    return np.ascontiguousarray(words), np.ascontiguousarray(byte.astype(np.uint8).reshape(k // 512, 16, n))


def unpack_weight(words, scales, fmt):
    g, p, n, _ = words.shape
    if fmt == "e4m3":
        vals = np.ascontiguousarray(words).view(ml_dtypes.float8_e4m3fn).astype(np.float64)
    else:
        nib = np.empty((g, p, n, 4), np.uint8)
        nib[..., 0::2] = words & 0xF
        nib[..., 1::2] = words >> 4
        vals = E2M1[nib]
    vals = vals * np.repeat(np.exp2(scales.astype(np.float64) - 127.0), 8, axis=1)[..., None]
    return vals.transpose(0, 1, 3, 2).reshape(g * 512, n)

def pack4(w):
    words, scales = pack_weight(w, "e2m1")
    return words.reshape(words.shape[0], 128, -1), scales


def unpack4(words, scales):
    return unpack_weight(words.reshape(words.shape[0], 128, -1, 2), scales, "e2m1")


B, Q_LEN, CTX, HID, H, KVH, D = 2, 128, 896, 2048, 16, 4, 128
T = CTX + Q_LEN
EPS = 1e-6
ROPE_BASE = 10000.0


def rms_norm(x, w):
    return x * (1.0 / np.sqrt(np.mean(x * x, axis=-1, keepdims=True) + EPS)) * w


def rotate_half(x):
    h = x.shape[-1] // 2
    return np.concatenate([-x[..., h:], x[..., :h]], axis=-1)


def setup_inputs():
    s = mx_kscale(HID)
    inv_freq = 1.0 / ROPE_BASE ** (np.arange(0, D, 2) / D)
    pos = np.random.randint(0, CTX, size=(B, 1)) + np.arange(T)[None, :]
    ang = pos[:, :, None] * inv_freq
    emb = np.concatenate([ang, ang], axis=-1)
    hidden_states = bf(np.random.standard_normal((B, Q_LEN, HID)) * s)
    target_hidden = bf(np.random.standard_normal((B, CTX, HID)) * s)
    Wq_words, Wq_scales = pack4((np.random.standard_normal((H * D, HID)) / np.sqrt(HID) / s[None, :]).T)
    Wk_words, Wk_scales = pack4((np.random.standard_normal((KVH * D, HID)) / np.sqrt(HID) / s[None, :]).T)
    Wv_words, Wv_scales = pack4((np.random.standard_normal((KVH * D, HID)) * 2.0 / np.sqrt(HID) / s[None, :]).T)
    return {"hidden_states": hidden_states,
            "target_hidden": target_hidden,
            "cos": bf(np.cos(emb)),
            "sin": bf(np.sin(emb)),
            "Wq_words": Wq_words,
            "Wq_scales": Wq_scales,
            "Wk_words": Wk_words,
            "Wk_scales": Wk_scales,
            "Wv_words": Wv_words,
            "Wv_scales": Wv_scales,
            "q_norm_w": bf(1.0 + 0.1 * np.random.standard_normal(D)),
            "k_norm_w": bf(1.0 + 0.1 * np.random.standard_normal(D))}


def reference(hidden_states, target_hidden, cos, sin, Wq_words, Wq_scales, Wk_words, Wk_scales, Wv_words, Wv_scales, q_norm_w, k_norm_w):
    kv_in = mxq(np.concatenate([f64(target_hidden), f64(hidden_states)], axis=1), 2, "e4m3")
    h_in = kv_in[:, CTX:, :]
    q = (h_in @ unpack4(Wq_words, Wq_scales)).reshape(B, Q_LEN, H, D)
    q = rms_norm(q, f64(q_norm_w)).transpose(0, 2, 1, 3)
    k = (kv_in @ unpack4(Wk_words, Wk_scales)).reshape(B, T, KVH, D)
    k = rms_norm(k, f64(k_norm_w)).transpose(0, 2, 1, 3)
    v = (kv_in @ unpack4(Wv_words, Wv_scales)).reshape(B, T, KVH, D).transpose(0, 2, 1, 3)
    c = f64(cos)[:, None, :, :]
    s = f64(sin)[:, None, :, :]
    q = q * c[:, :, -Q_LEN:, :] + rotate_half(q) * s[:, :, -Q_LEN:, :]
    k = k * c + rotate_half(k) * s
    return q, k, v

@@ -1,0 +1,294 @@
+from contextlib import ExitStack
+
+import concourse.mybir as mybir
+from concourse.masks import make_identity
+
+F32 = mybir.dt.float32
+BF16 = mybir.dt.bfloat16
+I32 = mybir.dt.int32
+U32 = mybir.dt.uint32
+U8 = mybir.dt.uint8
+FP8X4 = mybir.dt.float8_e4m3fn_x4
+FP4X4 = mybir.dt.float4_e2m1fn_x4
+ALU = mybir.AluOpType
+ACT = mybir.ActivationFunctionType
+
+P = 128
+BATCH = 2
+Q_LEN = 128
+CTX = 896
+HID = 2048
+Q_HEADS = 16
+KV_HEADS = 4
+HEAD_DIM = 128
+HALF = HEAD_DIM // 2
+EPS = 1e-6
+
+PACK = 4
+K_PASS = P * PACK
+PASSES = HID // K_PASS
+PASS_WORDS = K_PASS // 2
+UNIT_HEADS = 4
+UNIT_COLS = UNIT_HEADS * HEAD_DIM
+CTX_SLOTS = CTX // P
+SLOTS = CTX_SLOTS + 1
+ROUND_SLOTS = 2
+ROUNDS = SLOTS // ROUND_SLOTS
+assert ROUNDS == Q_HEADS // UNIT_HEADS
+
+FLOPS = 2 * HID * BATCH * ((CTX + Q_LEN) * 2 * KV_HEADS * HEAD_DIM + Q_LEN * Q_HEADS * HEAD_DIM)
+
+
+def context_rows(rows):
+    return rows.rearrange("(p i) w -> p i w", i=CTX_SLOTS)
+
+
+def slot_of_output(out, b, s):
+    if s == 0:
+        return out[b, :, CTX : CTX + Q_LEN, :].rearrange("h p d -> p h d")
+    return out[b, :, 0:CTX, :].rearrange("h (p i) d -> p h i d", i=CTX_SLOTS)[:, :, s - 1, :]
+
+
+def tile_dflashattention_pa_kernel(
+    tc,
+    hidden_states,
+    target_hidden,
+    cos,
+    sin,
+    Wq_words,
+    Wq_scales,
+    Wk_words,
+    Wk_scales,
+    Wv_words,
+    Wv_scales,
+    q_norm_w,
+    k_norm_w,
+    out_0,
+    out_1,
+    out_2,
+):
+    nc = tc.nc
+    rounds = [(b, c) for b in range(BATCH) for c in range(ROUNDS)]
+
+    with ExitStack() as ctx:
+        keep = ctx.enter_context(tc.tile_pool(name="keep", bufs=1))
+        stage = ctx.enter_context(tc.tile_pool(name="stage", bufs=3))
+        small = ctx.enter_context(tc.tile_pool(name="small", bufs=4))
+        rotated = ctx.enter_context(tc.tile_pool(name="rotated", bufs=5))
+        copied = ctx.enter_context(tc.tile_pool(name="copied", bufs=4))
+        xt_banks = ctx.enter_context(tc.psum_pool(name="xt_banks", bufs=4))
+        acc_banks = ctx.enter_context(tc.psum_pool(name="acc_banks", bufs=4))
+        ctx.enter_context(tc.manual_schedule())
+
+        x_tiles = {}
+        x_codes = {}
+        x_scales = {}
+        k_tables = {}
+        for b, c in rounds:
+            x_tiles[(b, c)] = keep.tile([P, ROUND_SLOTS, HID], BF16, name="x_%d_%d" % (b, c))
+            x_codes[(b, c)] = keep.tile(
+                [P, ROUND_SLOTS, PASSES * P], U32, name="x_codes_%d_%d" % (b, c), align_bytes=64
+            )
+            x_scales[(b, c)] = keep.tile(
+                [P, ROUND_SLOTS, PASSES * P], U8, name="x_scales_%d_%d" % (b, c), align_bytes=64
+            )
+            k_tables[(b, c)] = keep.tile([P, ROUND_SLOTS, 2, HEAD_DIM], F32, name="k_table_%d_%d" % (b, c))
+        q_tables = [keep.tile([P, 1, 2, HEAD_DIM], F32, name="q_table_%d" % b) for b in range(BATCH)]
+        cos_sb = [keep.tile([P, SLOTS, HEAD_DIM], BF16, name="cos_%d" % b) for b in range(BATCH)]
+        sin_sb = [keep.tile([P, SLOTS, HEAD_DIM], BF16, name="sin_%d" % b) for b in range(BATCH)]
+        wk_words = keep.tile([P, PASSES, 2 * UNIT_COLS], U8, name="wk_words", align_bytes=64)
+        wv_words = keep.tile([P, PASSES, 2 * UNIT_COLS], U8, name="wv_words", align_bytes=64)
+        wq_words = [
+            keep.tile([P, PASSES, 2 * UNIT_COLS], U8, name="wq_words_%d" % c, align_bytes=64) for c in range(ROUNDS)
+        ]
+        wk_scales = keep.tile([P, PASSES, UNIT_COLS], U8, name="wk_scales", align_bytes=64)
+        wv_scales = keep.tile([P, PASSES, UNIT_COLS], U8, name="wv_scales", align_bytes=64)
+        wq_scales = keep.tile([P, PASSES, ROUNDS * UNIT_COLS], U8, name="wq_scales", align_bytes=64)
+        k_gain = keep.tile([P, HEAD_DIM], BF16, name="k_gain")
+        q_gain = keep.tile([P, HEAD_DIM], BF16, name="q_gain")
+        identity = keep.tile([P, P], F32, name="identity")
+        eps = keep.tile([P, 1], F32, name="eps")
+        table_warmer = keep.tile([P, 1], F32, name="table_warmer")
+        squares = keep.tile([P, HEAD_DIM], F32, name="squares")
+
+        nc.vector.memset(eps[:], EPS)
+        for plane in (wk_scales, wq_scales, wv_scales):
+            nc.vector.memset(plane[:].bitcast(I32), 0)
+        make_identity(nc, identity[:])
+        nc.scalar.dma_start(out=k_gain[:], in_=k_norm_w.partition_broadcast(P))
+        nc.scalar.dma_start(out=q_gain[:], in_=q_norm_w.partition_broadcast(P))
+        nc.scalar.activation(out=table_warmer[:], in_=eps[:], func=ACT.Sqrt)
+
+        def load_x(b, c):
+            x_tile = x_tiles[(b, c)]
+            context = context_rows(target_hidden[b])
+            if c == 0:
+                nc.sync.dma_start(out=x_tile[:, 0, :], in_=hidden_states[b])
+                nc.sync.dma_start(out=x_tile[:, 1, :], in_=context[:, 0, :])
+            else:
+                first = ROUND_SLOTS * c - 1
+                nc.sync.dma_start(out=x_tile[:], in_=context[:, first : first + ROUND_SLOTS, :])
+
+        def load_words(words_sb, words, first_column):
+            first = first_column // 2
+            nc.sync.dma_start(
+                out=words_sb[:].bitcast(I32),
+                in_=words.bitcast(I32)[:, :, first : first + UNIT_COLS // 2].rearrange("g p n -> p g n"),
+            )
+
+        def load_scales(plane, scales):
+            for r in range(4):
+                nc.sync.dma_start(
+                    out=plane[r:P:32, :, :].bitcast(I32),
+                    in_=scales.bitcast(I32)[:, r:16:4, :].rearrange("g q n -> q g n"),
+                )
+
+        def load_angles(b):
+            for table_sb, table in ((cos_sb[b], cos), (sin_sb[b], sin)):
+                nc.sync.dma_start(out=table_sb[:, 0, :], in_=table[b, CTX : CTX + Q_LEN, :])
+                nc.sync.dma_start(out=table_sb[:, 1:SLOTS, :], in_=context_rows(table[b, 0:CTX, :]))
+
+        load_x(0, 0)
+        load_scales(wk_scales, Wk_scales)
+        load_words(wk_words, Wk_words, 0)
+        load_angles(0)
+        load_x(0, 1)
+        load_scales(wq_scales, Wq_scales)
+        load_words(wq_words[0], Wq_words, 0)
+        load_scales(wv_scales, Wv_scales)
+        load_words(wv_words, Wv_words, 0)
+        for c in range(2, ROUNDS):
+            load_x(0, c)
+            load_words(wq_words[c - 1], Wq_words, (c - 1) * UNIT_COLS)
+        load_words(wq_words[ROUNDS - 1], Wq_words, (ROUNDS - 1) * UNIT_COLS)
+        load_angles(1)
+        for c in range(ROUNDS):
+            load_x(1, c)
+
+        def make_table(table, cos_rows, sin_rows, gain):
+            count = table.shape[1]
+
+            def spread(columns):
+                return columns.unsqueeze(1).to_broadcast([P, count, columns.shape[1]])
+
+            nc.gpsimd.tensor_tensor(out=table[:, :, 0, :], in0=cos_rows, in1=spread(gain[:, :]), op=ALU.mult)
+            nc.gpsimd.tensor_tensor(
+                out=table[:, :, 1, 0:HALF], in0=sin_rows[:, :, HALF:HEAD_DIM], in1=spread(gain[:, 0:HALF]), op=ALU.mult
+            )
+            nc.gpsimd.tensor_tensor(
+                out=table[:, :, 1, HALF:HEAD_DIM], in0=sin_rows[:, :, 0:HALF], in1=spread(gain[:, HALF:HEAD_DIM]), op=ALU.mult
+            )
+
+        def make_tables(b, c):
+            first = ROUND_SLOTS * c
+            slots = slice(first, first + ROUND_SLOTS)
+            make_table(k_tables[(b, c)][:], cos_sb[b][:, slots, :], sin_sb[b][:, slots, :], k_gain)
+            if c == 0:
+                make_table(q_tables[b][:], cos_sb[b][:, 0:1, :], sin_sb[b][:, 0:1, :], q_gain)
+
+        def transpose_round(b, c):
+            banks = []
+            for j in range(ROUND_SLOTS):
+                words = x_tiles[(b, c)][:, j, :].bitcast(F32)
+                for first_pass in range(0, PASSES, 2):
+                    bank = xt_banks.tile([P, 2, 2, P], F32, name="xt")
+                    for i in range(2):
+                        start = (first_pass + i) * PASS_WORDS
+                        for u in range(2):
+                            nc.tensor.transpose(
+                                bank[:, i, u, :], words[:, start + u : start + PASS_WORDS : 2], identity[:]
+                            )
+                    banks.append(bank)
+            return banks
+
+        def quantise_round(b, c, banks):
+            for j in range(ROUND_SLOTS):
+                grouped = stage.tile([P, PASSES * P * PACK], BF16, name="grouped", align_bytes=64)
+                grouped_words = grouped[:].bitcast(F32).rearrange("p (g r u) -> p g r u", g=PASSES, u=2)
+                for half in range(2):
+                    nc.scalar.copy(
+                        out=grouped_words[:, 2 * half : 2 * half + 2, :, :],
+                        in_=banks[2 * j + half][:].rearrange("p g u r -> p g r u"),
+                    )
+                nc.vector.quantize_mx(
+                    out=x_codes[(b, c)][:, j, :].bitcast(FP8X4), scales=x_scales[(b, c)][:, j, :], in_=grouped[:]
+                )
+
+        def project(b, c, j, words_sb, plane, first_column):
+            acc = acc_banks.tile([P, UNIT_COLS], F32, name="acc")
+            for g in range(PASSES):
+                tokens = slice(g * P, (g + 1) * P)
+                nc.tensor.matmul_mx(
+                    out=acc[:],
+                    lhsT=x_codes[(b, c)][:, j, tokens].bitcast(FP8X4),
+                    lhsT_scale=x_scales[(b, c)][:, j, tokens],
+                    rhs=words_sb[:, g, :].bitcast(FP4X4),
+                    rhs_scale=plane[:, g, first_column : first_column + UNIT_COLS],
+                    start=(g == 0),
+                    stop=(g == PASSES - 1),
+                )
+            return acc
+
+        def norm_and_rotate(acc, table, destination):
+            sum_squares = small.tile([P, UNIT_HEADS], F32, name="sum_squares")
+            for h in range(UNIT_HEADS):
+                nc.scalar.activation(
+                    out=squares[:],
+                    in_=acc[:, h * HEAD_DIM : (h + 1) * HEAD_DIM],
+                    func=ACT.Square,
+                    accum_out=sum_squares[:, h : h + 1],
+                )
+            rms = small.tile([P, UNIT_HEADS], F32, name="rms")
+            nc.scalar.activation(out=rms[:], in_=sum_squares[:], func=ACT.Sqrt, scale=1.0 / HEAD_DIM, bias=eps[:])
+            inv_rms = small.tile([P, UNIT_HEADS], F32, name="inv_rms")
+            nc.vector.reciprocal(out=inv_rms[:], in_=rms[:])
+            products = rotated.tile([P, UNIT_HEADS, 2, HEAD_DIM], F32, name="products")
+            for h in range(UNIT_HEADS):
+                head = acc[:, h * HEAD_DIM : (h + 1) * HEAD_DIM]
+                nc.vector.scalar_tensor_tensor(
+                    out=products[:, h, :, :],
+                    in0=head.unsqueeze(1).to_broadcast([P, 2, HEAD_DIM]),
+                    scalar=inv_rms[:, h : h + 1],
+                    in1=table,
+                    op0=ALU.mult,
+                    op1=ALU.mult,
+                )
+            low = products[:, :, 0, 0:HALF]
+            high = products[:, :, 0, HALF:HEAD_DIM]
+            nc.gpsimd.tensor_tensor(out=low, in0=low, in1=products[:, :, 1, HALF:HEAD_DIM], op=ALU.subtract)
+            nc.gpsimd.tensor_tensor(out=high, in0=high, in1=products[:, :, 1, 0:HALF], op=ALU.add)
+            nc.sync.dma_start(out=destination, in_=products[:, :, 0, :])
+
+        def store_values(values, b, s):
+            nc.sync.dma_start(
+                out=slot_of_output(out_2, b, s), in_=values[:].rearrange("p (h d) -> p h d", h=KV_HEADS)
+            )
+
+        make_tables(0, 0)
+        quantise_round(0, 0, transpose_round(0, 0))
+        for n, (b, c) in enumerate(rounds):
+            following = rounds[n + 1] if n + 1 < len(rounds) else None
+            first_slot = ROUND_SLOTS * c
+
+            k_a = project(b, c, 0, wk_words, wk_scales, 0)
+            k_b = project(b, c, 1, wk_words, wk_scales, 0)
+            if following is not None:
+                banks = transpose_round(following[0], following[1])
+            norm_and_rotate(k_a, k_tables[(b, c)][:, 0, :, :], slot_of_output(out_1, b, first_slot))
+            norm_and_rotate(k_b, k_tables[(b, c)][:, 1, :, :], slot_of_output(out_1, b, first_slot + 1))
+            if following is not None:
+                make_tables(following[0], following[1])
+
+            q = project(b, 0, 0, wq_words[c], wq_scales, c * UNIT_COLS)
+            if following is not None:
+                quantise_round(following[0], following[1], banks)
+            v_a = project(b, c, 0, wv_words, wv_scales, 0)
+            v_b = project(b, c, 1, wv_words, wv_scales, 0)
+            heads = slice(c * UNIT_HEADS, (c + 1) * UNIT_HEADS)
+            norm_and_rotate(q, q_tables[b][:, 0, :, :], out_0[b, heads, :, :].rearrange("h p d -> p h d"))
+            values_a = copied.tile([P, UNIT_COLS], F32, name="values")
+            nc.scalar.copy(out=values_a[:], in_=v_a[:])
+            store_values(values_a, b, first_slot)
+            values_b = copied.tile([P, UNIT_COLS], F32, name="values")
+            nc.vector.tensor_copy(out=values_b[:], in_=v_b[:])
+            store_values(values_b, b, first_slot + 1)

@@ -35,6 +35,7 @@ SLOTS = CTX_SLOTS + 1
 ROUND_SLOTS = 2
 ROUNDS = SLOTS // ROUND_SLOTS
 assert ROUNDS == Q_HEADS // UNIT_HEADS
+LOADS_AHEAD = 3
 
 FLOPS = 2 * HID * BATCH * ((CTX + Q_LEN) * 2 * KV_HEADS * HEAD_DIM + Q_LEN * Q_HEADS * HEAD_DIM)
 
@@ -148,6 +149,13 @@ def tile_dflashattention_pa_kernel(
                 nc.sync.dma_start(out=table_sb[:, 0, :], in_=table[b, CTX : CTX + Q_LEN, :])
                 nc.sync.dma_start(out=table_sb[:, 1:SLOTS, :], in_=context_rows(table[b, 0:CTX, :]))
 
+        def load_round(b, c):
+            if c == 0:
+                load_angles(b)
+            load_x(b, c)
+            if b == 0:
+                load_words(wq_words[c], Wq_words, c * UNIT_COLS)
+
         load_x(0, 0)
         load_scales(wk_scales, Wk_scales)
         load_words(wk_words, Wk_words, 0)
@@ -157,13 +165,9 @@ def tile_dflashattention_pa_kernel(
         load_words(wq_words[0], Wq_words, 0)
         load_scales(wv_scales, Wv_scales)
         load_words(wv_words, Wv_words, 0)
-        for c in range(2, ROUNDS):
-            load_x(0, c)
-            load_words(wq_words[c - 1], Wq_words, (c - 1) * UNIT_COLS)
-        load_words(wq_words[ROUNDS - 1], Wq_words, (ROUNDS - 1) * UNIT_COLS)
-        load_angles(1)
-        for c in range(ROUNDS):
-            load_x(1, c)
+        load_words(wq_words[1], Wq_words, UNIT_COLS)
+        for b, c in rounds[2:LOADS_AHEAD]:
+            load_round(b, c)
 
         def make_table(table, cos_rows, sin_rows, gain):
             count = table.shape[1]
@@ -269,6 +273,8 @@ def tile_dflashattention_pa_kernel(
         for n, (b, c) in enumerate(rounds):
             following = rounds[n + 1] if n + 1 < len(rounds) else None
             first_slot = ROUND_SLOTS * c
+            if n + LOADS_AHEAD < len(rounds):
+                load_round(rounds[n + LOADS_AHEAD][0], rounds[n + LOADS_AHEAD][1])
 
             k_a = project(b, c, 0, wk_words, wk_scales, 0)
             k_b = project(b, c, 1, wk_words, wk_scales, 0)

@@ -105,19 +105,22 @@ def tile_dflashattention_pa_kernel(
         wk_scales = keep.tile([P, PASSES, UNIT_COLS], U8, name="wk_scales", align_bytes=64)
         wv_scales = keep.tile([P, PASSES, UNIT_COLS], U8, name="wv_scales", align_bytes=64)
         wq_scales = keep.tile([P, PASSES, ROUNDS * UNIT_COLS], U8, name="wq_scales", align_bytes=64)
-        k_gain = keep.tile([P, HEAD_DIM], BF16, name="k_gain")
-        q_gain = keep.tile([P, HEAD_DIM], BF16, name="q_gain")
+        gain_rows = keep.tile([P, 2 * HEAD_DIM], BF16, name="gain_rows")
+        ones = keep.tile([P, P], BF16, name="ones")
+        gains = keep.tile([P, 2 * HEAD_DIM], F32, name="gains")
+        k_gain = gains[:, 0:HEAD_DIM]
+        q_gain = gains[:, HEAD_DIM : 2 * HEAD_DIM]
         identity = keep.tile([P, P], F32, name="identity")
         eps = keep.tile([P, 1], F32, name="eps")
         table_warmer = keep.tile([P, 1], F32, name="table_warmer")
         squares = keep.tile([P, HEAD_DIM], F32, name="squares")
 
+        nc.vector.memset(gain_rows[:], 0.0)
+        nc.vector.memset(ones[:], 1.0)
         nc.vector.memset(eps[:], EPS)
         for plane in (wk_scales, wq_scales, wv_scales):
             nc.vector.memset(plane[:].bitcast(I32), 0)
         make_identity(nc, identity[:])
-        nc.scalar.dma_start(out=k_gain[:], in_=k_norm_w.partition_broadcast(P))
-        nc.scalar.dma_start(out=q_gain[:], in_=q_norm_w.partition_broadcast(P))
         nc.scalar.activation(out=table_warmer[:], in_=eps[:], func=ACT.Sqrt)
 
         def load_x(b, c):
@@ -137,11 +140,12 @@ def tile_dflashattention_pa_kernel(
                 in_=words.bitcast(I32)[:, :, first : first + UNIT_COLS // 2].rearrange("g p n -> p g n"),
             )
 
-        def load_scales(plane, scales):
+        def load_scales(plane, scales, first_column):
+            first = first_column // 4
             for r in range(4):
                 nc.sync.dma_start(
-                    out=plane[r:P:32, :, :].bitcast(I32),
-                    in_=scales.bitcast(I32)[:, r:16:4, :].rearrange("g q n -> q g n"),
+                    out=plane[r:P:32, :, first_column : first_column + UNIT_COLS].bitcast(I32),
+                    in_=scales.bitcast(I32)[:, r:16:4, first : first + UNIT_COLS // 4].rearrange("g q n -> q g n"),
                 )
 
         def load_angles(b):
@@ -154,20 +158,29 @@ def tile_dflashattention_pa_kernel(
                 load_angles(b)
             load_x(b, c)
             if b == 0:
-                load_words(wq_words[c], Wq_words, c * UNIT_COLS)
+                load_query_weight(c)
 
+        def load_query_weight(c):
+            load_scales(wq_scales, Wq_scales, c * UNIT_COLS)
+            load_words(wq_words[c], Wq_words, c * UNIT_COLS)
+
+        nc.sync.dma_start(out=gain_rows[0:1, 0:HEAD_DIM], in_=k_norm_w.unsqueeze(0))
+        nc.sync.dma_start(out=gain_rows[0:1, HEAD_DIM : 2 * HEAD_DIM], in_=q_norm_w.unsqueeze(0))
         load_x(0, 0)
-        load_scales(wk_scales, Wk_scales)
+        load_scales(wk_scales, Wk_scales, 0)
         load_words(wk_words, Wk_words, 0)
         load_angles(0)
         load_x(0, 1)
-        load_scales(wq_scales, Wq_scales)
-        load_words(wq_words[0], Wq_words, 0)
-        load_scales(wv_scales, Wv_scales)
+        load_query_weight(0)
+        load_scales(wv_scales, Wv_scales, 0)
         load_words(wv_words, Wv_words, 0)
-        load_words(wq_words[1], Wq_words, UNIT_COLS)
+        load_query_weight(1)
         for b, c in rounds[2:LOADS_AHEAD]:
             load_round(b, c)
+
+        spread_bank = acc_banks.tile([P, UNIT_COLS], F32, name="acc")
+        nc.tensor.matmul(out=spread_bank[:, 0 : 2 * HEAD_DIM], lhsT=ones[:], rhs=gain_rows[:], start=True, stop=True)
+        nc.scalar.copy(out=gains[:], in_=spread_bank[:, 0 : 2 * HEAD_DIM])
 
         def make_table(table, cos_rows, sin_rows, gain):
             count = table.shape[1]
@@ -175,7 +188,7 @@ def tile_dflashattention_pa_kernel(
             def spread(columns):
                 return columns.unsqueeze(1).to_broadcast([P, count, columns.shape[1]])
 
-            nc.gpsimd.tensor_tensor(out=table[:, :, 0, :], in0=cos_rows, in1=spread(gain[:, :]), op=ALU.mult)
+            nc.gpsimd.tensor_tensor(out=table[:, :, 0, :], in0=cos_rows, in1=spread(gain), op=ALU.mult)
             nc.gpsimd.tensor_tensor(
                 out=table[:, :, 1, 0:HALF], in0=sin_rows[:, :, HALF:HEAD_DIM], in1=spread(gain[:, 0:HALF]), op=ALU.mult
             )

@@ -44,12 +44,6 @@ def context_rows(rows):
     return rows.rearrange("(p i) w -> p i w", i=CTX_SLOTS)
 
 
-def slot_of_output(out, b, s):
-    if s == 0:
-        return out[b, :, CTX : CTX + Q_LEN, :].rearrange("h p d -> p h d")
-    return out[b, :, 0:CTX, :].rearrange("h (p i) d -> p h i d", i=CTX_SLOTS)[:, :, s - 1, :]
-
-
 def tile_dflashattention_pa_kernel(
     tc,
     hidden_states,
@@ -73,38 +67,39 @@ def tile_dflashattention_pa_kernel(
 
     with ExitStack() as ctx:
         keep = ctx.enter_context(tc.tile_pool(name="keep", bufs=1))
+        x_pool = ctx.enter_context(tc.tile_pool(name="x_pool", bufs=LOADS_AHEAD + 2))
+        table_pool = ctx.enter_context(tc.tile_pool(name="table_pool", bufs=3))
         stage = ctx.enter_context(tc.tile_pool(name="stage", bufs=3))
         small = ctx.enter_context(tc.tile_pool(name="small", bufs=4))
-        rotated = ctx.enter_context(tc.tile_pool(name="rotated", bufs=5))
-        copied = ctx.enter_context(tc.tile_pool(name="copied", bufs=4))
-        xt_banks = ctx.enter_context(tc.psum_pool(name="xt_banks", bufs=4))
-        acc_banks = ctx.enter_context(tc.psum_pool(name="acc_banks", bufs=4))
+        work = ctx.enter_context(tc.tile_pool(name="work", bufs=4))
+        done = ctx.enter_context(tc.tile_pool(name="done", bufs=3))
+        xt_banks = ctx.enter_context(tc.psum_pool(name="xt_banks", bufs=2))
+        acc_banks = ctx.enter_context(tc.psum_pool(name="acc_banks", bufs=6))
         ctx.enter_context(tc.manual_schedule())
 
         x_tiles = {}
+        k_tables = {}
         x_codes = {}
         x_scales = {}
-        k_tables = {}
         for b, c in rounds:
-            x_tiles[(b, c)] = keep.tile([P, ROUND_SLOTS, HID], BF16, name="x_%d_%d" % (b, c))
             x_codes[(b, c)] = keep.tile(
                 [P, ROUND_SLOTS, PASSES * P], U32, name="x_codes_%d_%d" % (b, c), align_bytes=64
             )
             x_scales[(b, c)] = keep.tile(
                 [P, ROUND_SLOTS, PASSES * P], U8, name="x_scales_%d_%d" % (b, c), align_bytes=64
             )
-            k_tables[(b, c)] = keep.tile([P, ROUND_SLOTS, 2, HEAD_DIM], F32, name="k_table_%d_%d" % (b, c))
         q_tables = [keep.tile([P, 1, 2, HEAD_DIM], F32, name="q_table_%d" % b) for b in range(BATCH)]
         cos_sb = [keep.tile([P, SLOTS, HEAD_DIM], BF16, name="cos_%d" % b) for b in range(BATCH)]
         sin_sb = [keep.tile([P, SLOTS, HEAD_DIM], BF16, name="sin_%d" % b) for b in range(BATCH)]
-        wk_words = keep.tile([P, PASSES, 2 * UNIT_COLS], U8, name="wk_words", align_bytes=64)
-        wv_words = keep.tile([P, PASSES, 2 * UNIT_COLS], U8, name="wv_words", align_bytes=64)
-        wq_words = [
-            keep.tile([P, PASSES, 2 * UNIT_COLS], U8, name="wq_words_%d" % c, align_bytes=64) for c in range(ROUNDS)
-        ]
-        wk_scales = keep.tile([P, PASSES, UNIT_COLS], U8, name="wk_scales", align_bytes=64)
-        wv_scales = keep.tile([P, PASSES, UNIT_COLS], U8, name="wv_scales", align_bytes=64)
-        wq_scales = keep.tile([P, PASSES, ROUNDS * UNIT_COLS], U8, name="wq_scales", align_bytes=64)
+
+        def weight_tiles(name):
+            words_sb = keep.tile([P, PASSES, 2 * UNIT_COLS], U8, name=name + "_words", align_bytes=64)
+            plane = keep.tile([P, PASSES, UNIT_COLS], U8, name=name + "_scales", align_bytes=64)
+            return words_sb, plane
+
+        wk = weight_tiles("wk")
+        wv = weight_tiles("wv")
+        wq = [weight_tiles("wq%d" % c) for c in range(ROUNDS)]
         gain_rows = keep.tile([P, 2 * HEAD_DIM], BF16, name="gain_rows")
         ones = keep.tile([P, P], BF16, name="ones")
         gains = keep.tile([P, 2 * HEAD_DIM], F32, name="gains")
@@ -118,13 +113,14 @@ def tile_dflashattention_pa_kernel(
         nc.vector.memset(gain_rows[:], 0.0)
         nc.vector.memset(ones[:], 1.0)
         nc.vector.memset(eps[:], EPS)
-        for plane in (wk_scales, wq_scales, wv_scales):
+        for words_sb, plane in [wk, wq[0], wv] + wq[1:]:
             nc.vector.memset(plane[:].bitcast(I32), 0)
         make_identity(nc, identity[:])
         nc.scalar.activation(out=table_warmer[:], in_=eps[:], func=ACT.Sqrt)
 
         def load_x(b, c):
-            x_tile = x_tiles[(b, c)]
+            x_tile = x_pool.tile([P, ROUND_SLOTS, HID], BF16, name="x")
+            x_tiles[(b, c)] = x_tile
             context = context_rows(target_hidden[b])
             if c == 0:
                 nc.sync.dma_start(out=x_tile[:, 0, :], in_=hidden_states[b])
@@ -133,20 +129,22 @@ def tile_dflashattention_pa_kernel(
                 first = ROUND_SLOTS * c - 1
                 nc.sync.dma_start(out=x_tile[:], in_=context[:, first : first + ROUND_SLOTS, :])
 
-        def load_words(words_sb, words, first_column):
+        def load_weight(tiles, words, scales, first_column):
+            words_sb, plane = tiles
+            first = first_column // 4
+            for r in range(4):
+                nc.sync.dma_start(
+                    out=plane[r:P:32, :, :].bitcast(I32),
+                    in_=scales.bitcast(I32)[:, r:16:4, first : first + UNIT_COLS // 4].rearrange("g q n -> q g n"),
+                )
             first = first_column // 2
             nc.sync.dma_start(
                 out=words_sb[:].bitcast(I32),
                 in_=words.bitcast(I32)[:, :, first : first + UNIT_COLS // 2].rearrange("g p n -> p g n"),
             )
 
-        def load_scales(plane, scales, first_column):
-            first = first_column // 4
-            for r in range(4):
-                nc.sync.dma_start(
-                    out=plane[r:P:32, :, first_column : first_column + UNIT_COLS].bitcast(I32),
-                    in_=scales.bitcast(I32)[:, r:16:4, first : first + UNIT_COLS // 4].rearrange("g q n -> q g n"),
-                )
+        def load_query_weight(c):
+            load_weight(wq[c], Wq_words, Wq_scales, c * UNIT_COLS)
 
         def load_angles(b):
             for table_sb, table in ((cos_sb[b], cos), (sin_sb[b], sin)):
@@ -160,27 +158,22 @@ def tile_dflashattention_pa_kernel(
             if b == 0:
                 load_query_weight(c)
 
-        def load_query_weight(c):
-            load_scales(wq_scales, Wq_scales, c * UNIT_COLS)
-            load_words(wq_words[c], Wq_words, c * UNIT_COLS)
-
         nc.sync.dma_start(out=gain_rows[0:1, 0:HEAD_DIM], in_=k_norm_w.unsqueeze(0))
         nc.sync.dma_start(out=gain_rows[0:1, HEAD_DIM : 2 * HEAD_DIM], in_=q_norm_w.unsqueeze(0))
         load_x(0, 0)
-        load_scales(wk_scales, Wk_scales, 0)
-        load_words(wk_words, Wk_words, 0)
+        load_weight(wk, Wk_words, Wk_scales, 0)
         load_angles(0)
         load_x(0, 1)
         load_query_weight(0)
-        load_scales(wv_scales, Wv_scales, 0)
-        load_words(wv_words, Wv_words, 0)
+        load_x(0, 2)
+        load_weight(wv, Wv_words, Wv_scales, 0)
         load_query_weight(1)
-        for b, c in rounds[2:LOADS_AHEAD]:
-            load_round(b, c)
+        load_query_weight(2)
 
-        spread_bank = acc_banks.tile([P, UNIT_COLS], F32, name="acc")
-        nc.tensor.matmul(out=spread_bank[:, 0 : 2 * HEAD_DIM], lhsT=ones[:], rhs=gain_rows[:], start=True, stop=True)
-        nc.scalar.copy(out=gains[:], in_=spread_bank[:, 0 : 2 * HEAD_DIM])
+        def spread_gains():
+            bank = acc_banks.tile([P, UNIT_COLS], F32, name="acc")
+            nc.tensor.matmul(out=bank[:, 0 : 2 * HEAD_DIM], lhsT=ones[:], rhs=gain_rows[:], start=True, stop=True)
+            nc.scalar.copy(out=gains[:], in_=bank[:, 0 : 2 * HEAD_DIM])
 
         def make_table(table, cos_rows, sin_rows, gain):
             count = table.shape[1]
@@ -188,50 +181,47 @@ def tile_dflashattention_pa_kernel(
             def spread(columns):
                 return columns.unsqueeze(1).to_broadcast([P, count, columns.shape[1]])
 
+            low = slice(0, HALF)
+            high = slice(HALF, HEAD_DIM)
             nc.gpsimd.tensor_tensor(out=table[:, :, 0, :], in0=cos_rows, in1=spread(gain), op=ALU.mult)
-            nc.gpsimd.tensor_tensor(
-                out=table[:, :, 1, 0:HALF], in0=sin_rows[:, :, HALF:HEAD_DIM], in1=spread(gain[:, 0:HALF]), op=ALU.mult
-            )
-            nc.gpsimd.tensor_tensor(
-                out=table[:, :, 1, HALF:HEAD_DIM], in0=sin_rows[:, :, 0:HALF], in1=spread(gain[:, HALF:HEAD_DIM]), op=ALU.mult
-            )
+            nc.gpsimd.tensor_tensor(out=table[:, :, 1, low], in0=sin_rows[:, :, high], in1=spread(gain[:, low]), op=ALU.mult)
+            nc.gpsimd.tensor_tensor(out=table[:, :, 1, high], in0=sin_rows[:, :, low], in1=spread(gain[:, high]), op=ALU.mult)
 
         def make_tables(b, c):
             first = ROUND_SLOTS * c
             slots = slice(first, first + ROUND_SLOTS)
-            make_table(k_tables[(b, c)][:], cos_sb[b][:, slots, :], sin_sb[b][:, slots, :], k_gain)
+            k_table = table_pool.tile([P, ROUND_SLOTS, 2, HEAD_DIM], F32, name="k_table")
+            k_tables[(b, c)] = k_table
+            make_table(k_table[:], cos_sb[b][:, slots, :], sin_sb[b][:, slots, :], k_gain)
             if c == 0:
                 make_table(q_tables[b][:], cos_sb[b][:, 0:1, :], sin_sb[b][:, 0:1, :], q_gain)
 
-        def transpose_round(b, c):
+        def transpose_slot(b, c, j):
+            words = x_tiles[(b, c)][:, j, :].bitcast(F32)
             banks = []
-            for j in range(ROUND_SLOTS):
-                words = x_tiles[(b, c)][:, j, :].bitcast(F32)
-                for first_pass in range(0, PASSES, 2):
-                    bank = xt_banks.tile([P, 2, 2, P], F32, name="xt")
-                    for i in range(2):
-                        start = (first_pass + i) * PASS_WORDS
-                        for u in range(2):
-                            nc.tensor.transpose(
-                                bank[:, i, u, :], words[:, start + u : start + PASS_WORDS : 2], identity[:]
-                            )
-                    banks.append(bank)
+            for first_pass in range(0, PASSES, 2):
+                bank = xt_banks.tile([P, 2, 2, P], F32, name="xt")
+                for i in range(2):
+                    start = (first_pass + i) * PASS_WORDS
+                    for u in range(2):
+                        nc.tensor.transpose(bank[:, i, u, :], words[:, start + u : start + PASS_WORDS : 2], identity[:])
+                banks.append(bank)
             return banks
 
-        def quantise_round(b, c, banks):
-            for j in range(ROUND_SLOTS):
-                grouped = stage.tile([P, PASSES * P * PACK], BF16, name="grouped", align_bytes=64)
-                grouped_words = grouped[:].bitcast(F32).rearrange("p (g r u) -> p g r u", g=PASSES, u=2)
-                for half in range(2):
-                    nc.scalar.copy(
-                        out=grouped_words[:, 2 * half : 2 * half + 2, :, :],
-                        in_=banks[2 * j + half][:].rearrange("p g u r -> p g r u"),
-                    )
-                nc.vector.quantize_mx(
-                    out=x_codes[(b, c)][:, j, :].bitcast(FP8X4), scales=x_scales[(b, c)][:, j, :], in_=grouped[:]
+        def quantise_slot(b, c, j, banks):
+            grouped = stage.tile([P, PASSES * P * PACK], BF16, name="grouped", align_bytes=64)
+            grouped_words = grouped[:].bitcast(F32).rearrange("p (g r u) -> p g r u", g=PASSES, u=2)
+            for half in range(2):
+                nc.scalar.copy(
+                    out=grouped_words[:, 2 * half : 2 * half + 2, :, :],
+                    in_=banks[half][:].rearrange("p g u r -> p g r u"),
                 )
+            nc.vector.quantize_mx(
+                out=x_codes[(b, c)][:, j, :].bitcast(FP8X4), scales=x_scales[(b, c)][:, j, :], in_=grouped[:]
+            )
 
-        def project(b, c, j, words_sb, plane, first_column):
+        def project(b, c, j, weight):
+            words_sb, plane = weight
             acc = acc_banks.tile([P, UNIT_COLS], F32, name="acc")
             for g in range(PASSES):
                 tokens = slice(g * P, (g + 1) * P)
@@ -240,13 +230,13 @@ def tile_dflashattention_pa_kernel(
                     lhsT=x_codes[(b, c)][:, j, tokens].bitcast(FP8X4),
                     lhsT_scale=x_scales[(b, c)][:, j, tokens],
                     rhs=words_sb[:, g, :].bitcast(FP4X4),
-                    rhs_scale=plane[:, g, first_column : first_column + UNIT_COLS],
+                    rhs_scale=plane[:, g, :],
                     start=(g == 0),
                     stop=(g == PASSES - 1),
                 )
             return acc
 
-        def norm_and_rotate(acc, table, destination):
+        def norm_and_rotate(acc, table, result, adder):
             sum_squares = small.tile([P, UNIT_HEADS], F32, name="sum_squares")
             for h in range(UNIT_HEADS):
                 nc.scalar.activation(
@@ -259,7 +249,7 @@ def tile_dflashattention_pa_kernel(
             nc.scalar.activation(out=rms[:], in_=sum_squares[:], func=ACT.Sqrt, scale=1.0 / HEAD_DIM, bias=eps[:])
             inv_rms = small.tile([P, UNIT_HEADS], F32, name="inv_rms")
             nc.vector.reciprocal(out=inv_rms[:], in_=rms[:])
-            products = rotated.tile([P, UNIT_HEADS, 2, HEAD_DIM], F32, name="products")
+            products = work.tile([P, UNIT_HEADS, 2, HEAD_DIM], F32, name="products")
             for h in range(UNIT_HEADS):
                 head = acc[:, h * HEAD_DIM : (h + 1) * HEAD_DIM]
                 nc.vector.scalar_tensor_tensor(
@@ -270,44 +260,66 @@ def tile_dflashattention_pa_kernel(
                     op0=ALU.mult,
                     op1=ALU.mult,
                 )
-            low = products[:, :, 0, 0:HALF]
-            high = products[:, :, 0, HALF:HEAD_DIM]
-            nc.gpsimd.tensor_tensor(out=low, in0=low, in1=products[:, :, 1, HALF:HEAD_DIM], op=ALU.subtract)
-            nc.gpsimd.tensor_tensor(out=high, in0=high, in1=products[:, :, 1, 0:HALF], op=ALU.add)
-            nc.sync.dma_start(out=destination, in_=products[:, :, 0, :])
+            low = slice(0, HALF)
+            high = slice(HALF, HEAD_DIM)
+            adder.tensor_tensor(out=result[:, :, low], in0=products[:, :, 0, low], in1=products[:, :, 1, high], op=ALU.subtract)
+            adder.tensor_tensor(out=result[:, :, high], in0=products[:, :, 0, high], in1=products[:, :, 1, low], op=ALU.add)
 
-        def store_values(values, b, s):
-            nc.sync.dma_start(
-                out=slot_of_output(out_2, b, s), in_=values[:].rearrange("p (h d) -> p h d", h=KV_HEADS)
-            )
+        def store_pair(pair, out, b, c):
+            context = out[b, :, 0:CTX, :].rearrange("h (p i) d -> p h i d", i=CTX_SLOTS)
+            if c == 0:
+                nc.sync.dma_start(out=out[b, :, CTX : CTX + Q_LEN, :].rearrange("h p d -> p h d"), in_=pair[:, :, 0, :])
+                nc.sync.dma_start(out=context[:, :, 0, :], in_=pair[:, :, 1, :])
+            else:
+                first = ROUND_SLOTS * c - 1
+                nc.sync.dma_start(out=context[:, :, first : first + ROUND_SLOTS, :], in_=pair[:])
 
-        make_tables(0, 0)
-        quantise_round(0, 0, transpose_round(0, 0))
-        for n, (b, c) in enumerate(rounds):
+        def key_units(n):
+            b, c = rounds[n]
             following = rounds[n + 1] if n + 1 < len(rounds) else None
-            first_slot = ROUND_SLOTS * c
-            if n + LOADS_AHEAD < len(rounds):
-                load_round(rounds[n + LOADS_AHEAD][0], rounds[n + LOADS_AHEAD][1])
-
-            k_a = project(b, c, 0, wk_words, wk_scales, 0)
-            k_b = project(b, c, 1, wk_words, wk_scales, 0)
-            if following is not None:
-                banks = transpose_round(following[0], following[1])
-            norm_and_rotate(k_a, k_tables[(b, c)][:, 0, :, :], slot_of_output(out_1, b, first_slot))
-            norm_and_rotate(k_b, k_tables[(b, c)][:, 1, :, :], slot_of_output(out_1, b, first_slot + 1))
+            keys = done.tile([P, KV_HEADS, ROUND_SLOTS, HEAD_DIM], F32, name="keys")
+            key_adders = (nc.vector, nc.gpsimd)
+            for j in range(ROUND_SLOTS):
+                k_acc = project(b, c, j, wk)
+                if following is not None:
+                    banks = transpose_slot(following[0], following[1], j)
+                norm_and_rotate(k_acc, k_tables[(b, c)][:, j, :, :], keys[:, :, j, :], key_adders[j])
+                if following is not None:
+                    quantise_slot(following[0], following[1], j, banks)
+            store_pair(keys, out_1, b, c)
             if following is not None:
                 make_tables(following[0], following[1])
 
-            q = project(b, 0, 0, wq_words[c], wq_scales, c * UNIT_COLS)
-            if following is not None:
-                quantise_round(following[0], following[1], banks)
-            v_a = project(b, c, 0, wv_words, wv_scales, 0)
-            v_b = project(b, c, 1, wv_words, wv_scales, 0)
-            heads = slice(c * UNIT_HEADS, (c + 1) * UNIT_HEADS)
-            norm_and_rotate(q, q_tables[b][:, 0, :, :], out_0[b, heads, :, :].rearrange("h p d -> p h d"))
-            values_a = copied.tile([P, UNIT_COLS], F32, name="values")
-            nc.scalar.copy(out=values_a[:], in_=v_a[:])
-            store_values(values_a, b, first_slot)
-            values_b = copied.tile([P, UNIT_COLS], F32, name="values")
-            nc.vector.tensor_copy(out=values_b[:], in_=v_b[:])
-            store_values(values_b, b, first_slot + 1)
+        def finish_query(n, q_acc):
+            b, c = rounds[n]
+            queries = done.tile([P, UNIT_HEADS, HEAD_DIM], F32, name="queries")
+            norm_and_rotate(q_acc, q_tables[b][:, 0, :, :], queries[:], nc.vector)
+            return queries
+
+        def finish_values(n, v_accs):
+            b, c = rounds[n]
+            values = done.tile([P, KV_HEADS, ROUND_SLOTS, HEAD_DIM], F32, name="values")
+            for j in range(ROUND_SLOTS):
+                nc.scalar.copy(out=values[:, :, j, :], in_=v_accs[j][:].rearrange("p (h d) -> p h d", h=KV_HEADS))
+            store_pair(values, out_2, b, c)
+
+        spread_gains()
+        make_tables(0, 0)
+        for j in range(ROUND_SLOTS):
+            quantise_slot(0, 0, j, transpose_slot(0, 0, j))
+        for n in range(len(rounds) + 1):
+            if n + LOADS_AHEAD < len(rounds):
+                load_round(rounds[n + LOADS_AHEAD][0], rounds[n + LOADS_AHEAD][1])
+            if n < len(rounds):
+                b, c = rounds[n]
+                key_units(n)
+                q_acc = project(b, 0, 0, wq[c])
+            if n > 0:
+                v_accs = [project(rounds[n - 1][0], rounds[n - 1][1], j, wv) for j in range(ROUND_SLOTS)]
+            if n < len(rounds):
+                queries = finish_query(n, q_acc)
+            if n > 0:
+                finish_values(n - 1, v_accs)
+            if n < len(rounds):
+                heads = slice(c * UNIT_HEADS, (c + 1) * UNIT_HEADS)
+                nc.sync.dma_start(out=out_0[b, heads, :, :].rearrange("h p d -> p h d"), in_=queries[:])

@@ -278,12 +278,11 @@ def tile_dflashattention_pa_kernel(
             b, c = rounds[n]
             following = rounds[n + 1] if n + 1 < len(rounds) else None
             keys = done.tile([P, KV_HEADS, ROUND_SLOTS, HEAD_DIM], F32, name="keys")
-            key_adders = (nc.vector, nc.gpsimd)
             for j in range(ROUND_SLOTS):
                 k_acc = project(b, c, j, wk)
                 if following is not None:
                     banks = transpose_slot(following[0], following[1], j)
-                norm_and_rotate(k_acc, k_tables[(b, c)][:, j, :, :], keys[:, :, j, :], key_adders[j])
+                norm_and_rotate(k_acc, k_tables[(b, c)][:, j, :, :], keys[:, :, j, :], nc.vector)
                 if following is not None:
                     quantise_slot(following[0], following[1], j, banks)
             store_pair(keys, out_1, b, c)
@@ -293,7 +292,7 @@ def tile_dflashattention_pa_kernel(
         def finish_query(n, q_acc):
             b, c = rounds[n]
             queries = done.tile([P, UNIT_HEADS, HEAD_DIM], F32, name="queries")
-            norm_and_rotate(q_acc, q_tables[b][:, 0, :, :], queries[:], nc.vector)
+            norm_and_rotate(q_acc, q_tables[b][:, 0, :, :], queries[:], nc.gpsimd)
             return queries
 
         def finish_values(n, v_accs):

@@ -73,8 +73,7 @@ def tile_dflashattention_pa_kernel(
         small = ctx.enter_context(tc.tile_pool(name="small", bufs=4))
         work = ctx.enter_context(tc.tile_pool(name="work", bufs=4))
         done = ctx.enter_context(tc.tile_pool(name="done", bufs=3))
-        xt_banks = ctx.enter_context(tc.psum_pool(name="xt_banks", bufs=2))
-        acc_banks = ctx.enter_context(tc.psum_pool(name="acc_banks", bufs=6))
+        banks_pool = ctx.enter_context(tc.psum_pool(name="banks_pool", bufs=8))
         ctx.enter_context(tc.manual_schedule())
 
         x_tiles = {}
@@ -171,7 +170,7 @@ def tile_dflashattention_pa_kernel(
         load_query_weight(2)
 
         def spread_gains():
-            bank = acc_banks.tile([P, UNIT_COLS], F32, name="acc")
+            bank = banks_pool.tile([P, UNIT_COLS], F32, name="bank")
             nc.tensor.matmul(out=bank[:, 0 : 2 * HEAD_DIM], lhsT=ones[:], rhs=gain_rows[:], start=True, stop=True)
             nc.scalar.copy(out=gains[:], in_=bank[:, 0 : 2 * HEAD_DIM])
 
@@ -200,7 +199,7 @@ def tile_dflashattention_pa_kernel(
             words = x_tiles[(b, c)][:, j, :].bitcast(F32)
             banks = []
             for first_pass in range(0, PASSES, 2):
-                bank = xt_banks.tile([P, 2, 2, P], F32, name="xt")
+                bank = banks_pool.tile([P, 2, 2, P], F32, name="bank")
                 for i in range(2):
                     start = (first_pass + i) * PASS_WORDS
                     for u in range(2):
@@ -208,7 +207,7 @@ def tile_dflashattention_pa_kernel(
                 banks.append(bank)
             return banks
 
-        def quantise_slot(b, c, j, banks):
+        def group_slot(banks):
             grouped = stage.tile([P, PASSES * P * PACK], BF16, name="grouped", align_bytes=64)
             grouped_words = grouped[:].bitcast(F32).rearrange("p (g r u) -> p g r u", g=PASSES, u=2)
             for half in range(2):
@@ -216,13 +215,16 @@ def tile_dflashattention_pa_kernel(
                     out=grouped_words[:, 2 * half : 2 * half + 2, :, :],
                     in_=banks[half][:].rearrange("p g u r -> p g r u"),
                 )
+            return grouped
+
+        def quantise_slot(b, c, j, grouped):
             nc.vector.quantize_mx(
                 out=x_codes[(b, c)][:, j, :].bitcast(FP8X4), scales=x_scales[(b, c)][:, j, :], in_=grouped[:]
             )
 
         def project(b, c, j, weight):
             words_sb, plane = weight
-            acc = acc_banks.tile([P, UNIT_COLS], F32, name="acc")
+            acc = banks_pool.tile([P, UNIT_COLS], F32, name="bank")
             for g in range(PASSES):
                 tokens = slice(g * P, (g + 1) * P)
                 nc.tensor.matmul_mx(
@@ -236,7 +238,7 @@ def tile_dflashattention_pa_kernel(
                 )
             return acc
 
-        def norm_and_rotate(acc, table, result, adder):
+        def root_mean_squares(acc):
             sum_squares = small.tile([P, UNIT_HEADS], F32, name="sum_squares")
             for h in range(UNIT_HEADS):
                 nc.scalar.activation(
@@ -247,6 +249,9 @@ def tile_dflashattention_pa_kernel(
                 )
             rms = small.tile([P, UNIT_HEADS], F32, name="rms")
             nc.scalar.activation(out=rms[:], in_=sum_squares[:], func=ACT.Sqrt, scale=1.0 / HEAD_DIM, bias=eps[:])
+            return rms
+
+        def norm_and_rotate(acc, rms, table, result, adder):
             inv_rms = small.tile([P, UNIT_HEADS], F32, name="inv_rms")
             nc.vector.reciprocal(out=inv_rms[:], in_=rms[:])
             products = work.tile([P, UNIT_HEADS, 2, HEAD_DIM], F32, name="products")
@@ -278,13 +283,16 @@ def tile_dflashattention_pa_kernel(
             b, c = rounds[n]
             following = rounds[n + 1] if n + 1 < len(rounds) else None
             keys = done.tile([P, KV_HEADS, ROUND_SLOTS, HEAD_DIM], F32, name="keys")
+            k_accs = [project(b, c, j, wk) for j in range(ROUND_SLOTS)]
+            if following is not None:
+                banks = [transpose_slot(following[0], following[1], j) for j in range(ROUND_SLOTS)]
+            k_rms = [root_mean_squares(k_accs[j]) for j in range(ROUND_SLOTS)]
+            if following is not None:
+                grouped = [group_slot(banks[j]) for j in range(ROUND_SLOTS)]
             for j in range(ROUND_SLOTS):
-                k_acc = project(b, c, j, wk)
+                norm_and_rotate(k_accs[j], k_rms[j], k_tables[(b, c)][:, j, :, :], keys[:, :, j, :], nc.vector)
                 if following is not None:
-                    banks = transpose_slot(following[0], following[1], j)
-                norm_and_rotate(k_acc, k_tables[(b, c)][:, j, :, :], keys[:, :, j, :], nc.vector)
-                if following is not None:
-                    quantise_slot(following[0], following[1], j, banks)
+                    quantise_slot(following[0], following[1], j, grouped[j])
             store_pair(keys, out_1, b, c)
             if following is not None:
                 make_tables(following[0], following[1])
@@ -292,7 +300,7 @@ def tile_dflashattention_pa_kernel(
         def finish_query(n, q_acc):
             b, c = rounds[n]
             queries = done.tile([P, UNIT_HEADS, HEAD_DIM], F32, name="queries")
-            norm_and_rotate(q_acc, q_tables[b][:, 0, :, :], queries[:], nc.gpsimd)
+            norm_and_rotate(q_acc, root_mean_squares(q_acc), q_tables[b][:, 0, :, :], queries[:], nc.gpsimd)
             return queries
 
         def finish_values(n, v_accs):
@@ -304,8 +312,9 @@ def tile_dflashattention_pa_kernel(
 
         spread_gains()
         make_tables(0, 0)
+        first_banks = [transpose_slot(0, 0, j) for j in range(ROUND_SLOTS)]
         for j in range(ROUND_SLOTS):
-            quantise_slot(0, 0, j, transpose_slot(0, 0, j))
+            quantise_slot(0, 0, j, group_slot(first_banks[j]))
         for n in range(len(rounds) + 1):
             if n + LOADS_AHEAD < len(rounds):
                 load_round(rounds[n + LOADS_AHEAD][0], rounds[n + LOADS_AHEAD][1])

@@ -35,6 +35,7 @@ SLOTS = CTX_SLOTS + 1
 ROUND_SLOTS = 2
 ROUNDS = SLOTS // ROUND_SLOTS
 assert ROUNDS == Q_HEADS // UNIT_HEADS
+FIRST_PIECES = 2
 LOADS_AHEAD = 3
 
 FLOPS = 2 * HID * BATCH * ((CTX + Q_LEN) * 2 * KV_HEADS * HEAD_DIM + Q_LEN * Q_HEADS * HEAD_DIM)
@@ -71,7 +72,7 @@ def tile_dflashattention_pa_kernel(
         table_pool = ctx.enter_context(tc.tile_pool(name="table_pool", bufs=3))
         stage = ctx.enter_context(tc.tile_pool(name="stage", bufs=3))
         small = ctx.enter_context(tc.tile_pool(name="small", bufs=4))
-        work = ctx.enter_context(tc.tile_pool(name="work", bufs=4))
+        work = ctx.enter_context(tc.tile_pool(name="work", bufs=2))
         done = ctx.enter_context(tc.tile_pool(name="done", bufs=3))
         banks_pool = ctx.enter_context(tc.psum_pool(name="banks_pool", bufs=8))
         ctx.enter_context(tc.manual_schedule())
@@ -102,8 +103,9 @@ def tile_dflashattention_pa_kernel(
         gain_rows = keep.tile([P, 2 * HEAD_DIM], BF16, name="gain_rows")
         ones = keep.tile([P, P], BF16, name="ones")
         gains = keep.tile([P, 2 * HEAD_DIM], F32, name="gains")
-        k_gain = gains[:, 0:HEAD_DIM]
-        q_gain = gains[:, HEAD_DIM : 2 * HEAD_DIM]
+        minus_gains = keep.tile([P, 2 * HEAD_DIM], F32, name="minus_gains")
+        k_gain = (gains[:, 0:HEAD_DIM], minus_gains[:, 0:HEAD_DIM])
+        q_gain = (gains[:, HEAD_DIM : 2 * HEAD_DIM], minus_gains[:, HEAD_DIM : 2 * HEAD_DIM])
         identity = keep.tile([P, P], F32, name="identity")
         eps = keep.tile([P, 1], F32, name="eps")
         table_warmer = keep.tile([P, 1], F32, name="table_warmer")
@@ -115,15 +117,19 @@ def tile_dflashattention_pa_kernel(
         for words_sb, plane in [wk, wq[0], wv] + wq[1:]:
             nc.vector.memset(plane[:].bitcast(I32), 0)
         make_identity(nc, identity[:])
-        nc.scalar.activation(out=table_warmer[:], in_=eps[:], func=ACT.Sqrt)
+        nc.scalar.activation(out=table_warmer[:], in_=eps[:], func=ACT.Abs_reciprocal_sqrt)
 
         def load_x(b, c):
             x_tile = x_pool.tile([P, ROUND_SLOTS, HID], BF16, name="x")
             x_tiles[(b, c)] = x_tile
             context = context_rows(target_hidden[b])
             if c == 0:
-                nc.sync.dma_start(out=x_tile[:, 0, :], in_=hidden_states[b])
-                nc.sync.dma_start(out=x_tile[:, 1, :], in_=context[:, 0, :])
+                pieces = FIRST_PIECES if b == 0 else 1
+                width = HID // pieces
+                for rows, j in ((hidden_states[b], 0), (context[:, 0, :], 1)):
+                    for i in range(pieces):
+                        columns = slice(i * width, (i + 1) * width)
+                        nc.sync.dma_start(out=x_tile[:, j, columns], in_=rows[:, columns])
             else:
                 first = ROUND_SLOTS * c - 1
                 nc.sync.dma_start(out=x_tile[:], in_=context[:, first : first + ROUND_SLOTS, :])
@@ -157,9 +163,9 @@ def tile_dflashattention_pa_kernel(
             if b == 0:
                 load_query_weight(c)
 
+        load_x(0, 0)
         nc.sync.dma_start(out=gain_rows[0:1, 0:HEAD_DIM], in_=k_norm_w.unsqueeze(0))
         nc.sync.dma_start(out=gain_rows[0:1, HEAD_DIM : 2 * HEAD_DIM], in_=q_norm_w.unsqueeze(0))
-        load_x(0, 0)
         load_weight(wk, Wk_words, Wk_scales, 0)
         load_angles(0)
         load_x(0, 1)
@@ -172,10 +178,15 @@ def tile_dflashattention_pa_kernel(
         def spread_gains():
             bank = banks_pool.tile([P, UNIT_COLS], F32, name="bank")
             nc.tensor.matmul(out=bank[:, 0 : 2 * HEAD_DIM], lhsT=ones[:], rhs=gain_rows[:], start=True, stop=True)
+            return bank
+
+        def keep_gains(bank):
             nc.scalar.copy(out=gains[:], in_=bank[:, 0 : 2 * HEAD_DIM])
+            nc.scalar.mul(out=minus_gains[:], in_=bank[:, 0 : 2 * HEAD_DIM], mul=-1.0)
 
         def make_table(table, cos_rows, sin_rows, gain):
             count = table.shape[1]
+            gain, minus_gain = gain
 
             def spread(columns):
                 return columns.unsqueeze(1).to_broadcast([P, count, columns.shape[1]])
@@ -184,7 +195,7 @@ def tile_dflashattention_pa_kernel(
             high = slice(HALF, HEAD_DIM)
             nc.gpsimd.tensor_tensor(out=table[:, :, 0, :], in0=cos_rows, in1=spread(gain), op=ALU.mult)
             nc.gpsimd.tensor_tensor(out=table[:, :, 1, low], in0=sin_rows[:, :, high], in1=spread(gain[:, low]), op=ALU.mult)
-            nc.gpsimd.tensor_tensor(out=table[:, :, 1, high], in0=sin_rows[:, :, low], in1=spread(gain[:, high]), op=ALU.mult)
+            nc.gpsimd.tensor_tensor(out=table[:, :, 1, high], in0=sin_rows[:, :, low], in1=spread(minus_gain[:, high]), op=ALU.mult)
 
         def make_tables(b, c):
             first = ROUND_SLOTS * c
@@ -238,23 +249,24 @@ def tile_dflashattention_pa_kernel(
                 )
             return acc
 
-        def root_mean_squares(acc):
-            sum_squares = small.tile([P, UNIT_HEADS], F32, name="sum_squares")
-            for h in range(UNIT_HEADS):
-                nc.scalar.activation(
-                    out=squares[:],
-                    in_=acc[:, h * HEAD_DIM : (h + 1) * HEAD_DIM],
-                    func=ACT.Square,
-                    accum_out=sum_squares[:, h : h + 1],
-                )
-            rms = small.tile([P, UNIT_HEADS], F32, name="rms")
-            nc.scalar.activation(out=rms[:], in_=sum_squares[:], func=ACT.Sqrt, scale=1.0 / HEAD_DIM, bias=eps[:])
-            return rms
+        def inverse_rms(accs):
+            count = len(accs) * UNIT_HEADS
+            sum_squares = small.tile([P, count], F32, name="sum_squares")
+            for i in range(len(accs)):
+                for h in range(UNIT_HEADS):
+                    nc.scalar.activation(
+                        out=squares[:],
+                        in_=accs[i][:, h * HEAD_DIM : (h + 1) * HEAD_DIM],
+                        func=ACT.Square,
+                        accum_out=sum_squares[:, i * UNIT_HEADS + h : i * UNIT_HEADS + h + 1],
+                    )
+            inv_rms = small.tile([P, count], F32, name="inv_rms")
+            nc.scalar.activation(
+                out=inv_rms[:], in_=sum_squares[:], func=ACT.Abs_reciprocal_sqrt, scale=1.0 / HEAD_DIM, bias=eps[:]
+            )
+            return inv_rms
 
-        def norm_and_rotate(acc, rms, table, result, adder):
-            inv_rms = small.tile([P, UNIT_HEADS], F32, name="inv_rms")
-            nc.vector.reciprocal(out=inv_rms[:], in_=rms[:])
-            products = work.tile([P, UNIT_HEADS, 2, HEAD_DIM], F32, name="products")
+        def norm_and_scale(acc, inv_rms, table, products):
             for h in range(UNIT_HEADS):
                 head = acc[:, h * HEAD_DIM : (h + 1) * HEAD_DIM]
                 nc.vector.scalar_tensor_tensor(
@@ -265,42 +277,71 @@ def tile_dflashattention_pa_kernel(
                     op0=ALU.mult,
                     op1=ALU.mult,
                 )
-            low = slice(0, HALF)
-            high = slice(HALF, HEAD_DIM)
-            adder.tensor_tensor(out=result[:, :, low], in0=products[:, :, 0, low], in1=products[:, :, 1, high], op=ALU.subtract)
-            adder.tensor_tensor(out=result[:, :, high], in0=products[:, :, 0, high], in1=products[:, :, 1, low], op=ALU.add)
+
+        def rotate(products, result, adder):
+            halves = "p r (s j) -> p r s j"
+            adder.tensor_tensor(
+                out=result.rearrange(halves, s=2),
+                in0=products[:, :, 0, :].rearrange(halves, s=2),
+                in1=products[:, :, 1, :].rearrange(halves, s=2)[:, :, ::-1, :],
+                op=ALU.add,
+            )
+
+        def store_slot(pair, out, b, c, j):
+            slot = ROUND_SLOTS * c + j
+            if slot == 0:
+                rows = out[b, :, CTX : CTX + Q_LEN, :].rearrange("h p d -> p h d")
+            else:
+                rows = out[b, :, 0:CTX, :].rearrange("h (p i) d -> p h i d", i=CTX_SLOTS)[:, :, slot - 1, :]
+            nc.sync.dma_start(out=rows, in_=pair[:, :, j, :])
 
         def store_pair(pair, out, b, c):
-            context = out[b, :, 0:CTX, :].rearrange("h (p i) d -> p h i d", i=CTX_SLOTS)
             if c == 0:
-                nc.sync.dma_start(out=out[b, :, CTX : CTX + Q_LEN, :].rearrange("h p d -> p h d"), in_=pair[:, :, 0, :])
-                nc.sync.dma_start(out=context[:, :, 0, :], in_=pair[:, :, 1, :])
+                for j in range(ROUND_SLOTS):
+                    store_slot(pair, out, b, c, j)
             else:
                 first = ROUND_SLOTS * c - 1
-                nc.sync.dma_start(out=context[:, :, first : first + ROUND_SLOTS, :], in_=pair[:])
+                context = out[b, :, 0:CTX, :].rearrange("h (p i) d -> p h i d", i=CTX_SLOTS)
+                nc.sync.dma_start(out=context[:, :, first : first + ROUND_SLOTS, :], in_=pair)
 
         def key_units(n):
             b, c = rounds[n]
             following = rounds[n + 1] if n + 1 < len(rounds) else None
-            keys = done.tile([P, KV_HEADS, ROUND_SLOTS, HEAD_DIM], F32, name="keys")
+            keys = done.tile([P, KV_HEADS * ROUND_SLOTS, HEAD_DIM], F32, name="keys")
             k_accs = [project(b, c, j, wk) for j in range(ROUND_SLOTS)]
             if following is not None:
                 banks = [transpose_slot(following[0], following[1], j) for j in range(ROUND_SLOTS)]
-            k_rms = [root_mean_squares(k_accs[j]) for j in range(ROUND_SLOTS)]
-            if following is not None:
-                grouped = [group_slot(banks[j]) for j in range(ROUND_SLOTS)]
+            products = work.tile([P, KV_HEADS * ROUND_SLOTS, 2, HEAD_DIM], F32, name="k_products")
+            pair = keys[:].rearrange("p (h i) d -> p h i d", i=ROUND_SLOTS)
+            slot_rows = [slice(j, KV_HEADS * ROUND_SLOTS, ROUND_SLOTS) for j in range(ROUND_SLOTS)]
+            if following is None:
+                for j in range(ROUND_SLOTS):
+                    norm_and_scale(
+                        k_accs[j], inverse_rms([k_accs[j]]), k_tables[(b, c)][:, j, :, :], products[:, slot_rows[j], :, :]
+                    )
+                    rotate(products[:, slot_rows[j], :, :], keys[:, slot_rows[j], :], nc.vector)
+                    store_slot(pair, out_1, b, c, j)
+                return
+            inv_rms = inverse_rms(k_accs)
+            grouped = [group_slot(banks[j]) for j in range(ROUND_SLOTS)]
             for j in range(ROUND_SLOTS):
-                norm_and_rotate(k_accs[j], k_rms[j], k_tables[(b, c)][:, j, :, :], keys[:, :, j, :], nc.vector)
-                if following is not None:
-                    quantise_slot(following[0], following[1], j, grouped[j])
-            store_pair(keys, out_1, b, c)
-            if following is not None:
-                make_tables(following[0], following[1])
+                norm_and_scale(
+                    k_accs[j],
+                    inv_rms[:, j * UNIT_HEADS : (j + 1) * UNIT_HEADS],
+                    k_tables[(b, c)][:, j, :, :],
+                    products[:, slot_rows[j], :, :],
+                )
+                quantise_slot(following[0], following[1], j, grouped[j])
+            rotate(products, keys[:], nc.vector)
+            store_pair(pair, out_1, b, c)
+            make_tables(following[0], following[1])
 
         def finish_query(n, q_acc):
             b, c = rounds[n]
             queries = done.tile([P, UNIT_HEADS, HEAD_DIM], F32, name="queries")
-            norm_and_rotate(q_acc, root_mean_squares(q_acc), q_tables[b][:, 0, :, :], queries[:], nc.gpsimd)
+            products = work.tile([P, UNIT_HEADS, 2, HEAD_DIM], F32, name="q_products")
+            norm_and_scale(q_acc, inverse_rms([q_acc]), q_tables[b][:, 0, :, :], products)
+            rotate(products, queries[:], nc.gpsimd)
             return queries
 
         def finish_values(n, v_accs):
@@ -308,26 +349,39 @@ def tile_dflashattention_pa_kernel(
             values = done.tile([P, KV_HEADS, ROUND_SLOTS, HEAD_DIM], F32, name="values")
             for j in range(ROUND_SLOTS):
                 nc.scalar.copy(out=values[:, :, j, :], in_=v_accs[j][:].rearrange("p (h d) -> p h d", h=KV_HEADS))
-            store_pair(values, out_2, b, c)
+                if n == len(rounds) - 1:
+                    store_slot(values[:], out_2, b, c, j)
+            if n < len(rounds) - 1:
+                store_pair(values[:], out_2, b, c)
 
-        spread_gains()
+        def store_queries(n, queries):
+            b, c = rounds[n]
+            heads = slice(c * UNIT_HEADS, (c + 1) * UNIT_HEADS)
+            nc.sync.dma_start(out=out_0[b, heads, :, :].rearrange("h p d -> p h d"), in_=queries[:])
+
+        first_banks = [transpose_slot(0, 0, 0)]
+        gains_bank = spread_gains()
+        first_banks.append(transpose_slot(0, 0, 1))
+        quantise_slot(0, 0, 0, group_slot(first_banks[0]))
+        keep_gains(gains_bank)
         make_tables(0, 0)
-        first_banks = [transpose_slot(0, 0, j) for j in range(ROUND_SLOTS)]
-        for j in range(ROUND_SLOTS):
-            quantise_slot(0, 0, j, group_slot(first_banks[j]))
+        quantise_slot(0, 0, 1, group_slot(first_banks[1]))
         for n in range(len(rounds) + 1):
             if n + LOADS_AHEAD < len(rounds):
                 load_round(rounds[n + LOADS_AHEAD][0], rounds[n + LOADS_AHEAD][1])
+            last = n == len(rounds) - 1
             if n < len(rounds):
                 b, c = rounds[n]
+                if last:
+                    store_queries(n, finish_query(n, project(b, 0, 0, wq[c])))
                 key_units(n)
-                q_acc = project(b, 0, 0, wq[c])
+                if not last:
+                    q_acc = project(b, 0, 0, wq[c])
             if n > 0:
                 v_accs = [project(rounds[n - 1][0], rounds[n - 1][1], j, wv) for j in range(ROUND_SLOTS)]
-            if n < len(rounds):
+            if n < len(rounds) - 1:
                 queries = finish_query(n, q_acc)
             if n > 0:
                 finish_values(n - 1, v_accs)
-            if n < len(rounds):
-                heads = slice(c * UNIT_HEADS, (c + 1) * UNIT_HEADS)
-                nc.sync.dma_start(out=out_0[b, heads, :, :].rearrange("h p d -> p h d"), in_=queries[:])
+            if n < len(rounds) - 1:
+                store_queries(n, queries)

@@ -110,9 +110,11 @@ def tile_dflashattention_pa_kernel(
         eps = keep.tile([P, 1], F32, name="eps")
         table_warmer = keep.tile([P, 1], F32, name="table_warmer")
         squares = keep.tile([P, HEAD_DIM], F32, name="squares")
+        idle_rows = keep.tile([P, UNIT_COLS], BF16, name="idle_rows")
 
-        nc.vector.memset(gain_rows[:], 0.0)
         nc.vector.memset(ones[:], 1.0)
+        nc.vector.memset(idle_rows[:], 0.0)
+        nc.vector.memset(gain_rows[:], 0.0)
         nc.vector.memset(eps[:], EPS)
         for words_sb, plane in [wk, wq[0], wv] + wq[1:]:
             nc.vector.memset(plane[:].bitcast(I32), 0)
@@ -151,14 +153,19 @@ def tile_dflashattention_pa_kernel(
         def load_query_weight(c):
             load_weight(wq[c], Wq_words, Wq_scales, c * UNIT_COLS)
 
-        def load_angles(b):
+        def load_first_angles(b):
             for table_sb, table in ((cos_sb[b], cos), (sin_sb[b], sin)):
                 nc.sync.dma_start(out=table_sb[:, 0, :], in_=table[b, CTX : CTX + Q_LEN, :])
-                nc.sync.dma_start(out=table_sb[:, 1:SLOTS, :], in_=context_rows(table[b, 0:CTX, :]))
+                nc.sync.dma_start(out=table_sb[:, 1, :], in_=context_rows(table[b, 0:CTX, :])[:, 0, :])
+
+        def load_other_angles(b):
+            for table_sb, table in ((cos_sb[b], cos), (sin_sb[b], sin)):
+                nc.sync.dma_start(out=table_sb[:, 2:SLOTS, :], in_=context_rows(table[b, 0:CTX, :])[:, 1:CTX_SLOTS, :])
 
         def load_round(b, c):
             if c == 0:
-                load_angles(b)
+                load_first_angles(b)
+                load_other_angles(b)
             load_x(b, c)
             if b == 0:
                 load_query_weight(c)
@@ -167,8 +174,9 @@ def tile_dflashattention_pa_kernel(
         nc.sync.dma_start(out=gain_rows[0:1, 0:HEAD_DIM], in_=k_norm_w.unsqueeze(0))
         nc.sync.dma_start(out=gain_rows[0:1, HEAD_DIM : 2 * HEAD_DIM], in_=q_norm_w.unsqueeze(0))
         load_weight(wk, Wk_words, Wk_scales, 0)
-        load_angles(0)
+        load_first_angles(0)
         load_x(0, 1)
+        load_other_angles(0)
         load_query_weight(0)
         load_x(0, 2)
         load_weight(wv, Wv_words, Wv_scales, 0)
@@ -359,9 +367,18 @@ def tile_dflashattention_pa_kernel(
             heads = slice(c * UNIT_HEADS, (c + 1) * UNIT_HEADS)
             nc.sync.dma_start(out=out_0[b, heads, :, :].rearrange("h p d -> p h d"), in_=queries[:])
 
+        idle_bank = banks_pool.tile([P, UNIT_COLS], F32, name="bank")
+
+        def keep_busy(count):
+            for i in range(count):
+                nc.tensor.matmul(out=idle_bank[:], lhsT=ones[:], rhs=idle_rows[:], start=True, stop=True)
+
+        keep_busy(4)
         first_banks = [transpose_slot(0, 0, 0)]
         gains_bank = spread_gains()
+        keep_busy(2)
         first_banks.append(transpose_slot(0, 0, 1))
+        keep_busy(3)
         quantise_slot(0, 0, 0, group_slot(first_banks[0]))
         keep_gains(gains_bank)
         make_tables(0, 0)

@@ -36,6 +36,7 @@ ROUND_SLOTS = 2
 ROUNDS = SLOTS // ROUND_SLOTS
 assert ROUNDS == Q_HEADS // UNIT_HEADS
 FIRST_PIECES = 2
+ORDER_AHEAD = 2
 LOADS_AHEAD = 3
 
 FLOPS = 2 * HID * BATCH * ((CTX + Q_LEN) * 2 * KV_HEADS * HEAD_DIM + Q_LEN * Q_HEADS * HEAD_DIM)
@@ -69,6 +70,7 @@ def tile_dflashattention_pa_kernel(
     with ExitStack() as ctx:
         keep = ctx.enter_context(tc.tile_pool(name="keep", bufs=1))
         x_pool = ctx.enter_context(tc.tile_pool(name="x_pool", bufs=LOADS_AHEAD + 2))
+        order_pool = ctx.enter_context(tc.tile_pool(name="order_pool", bufs=2))
         table_pool = ctx.enter_context(tc.tile_pool(name="table_pool", bufs=3))
         stage = ctx.enter_context(tc.tile_pool(name="stage", bufs=3))
         small = ctx.enter_context(tc.tile_pool(name="small", bufs=4))
@@ -78,6 +80,7 @@ def tile_dflashattention_pa_kernel(
         ctx.enter_context(tc.manual_schedule())
 
         x_tiles = {}
+        ordered_words = {}
         k_tables = {}
         x_codes = {}
         x_scales = {}
@@ -214,15 +217,27 @@ def tile_dflashattention_pa_kernel(
             if c == 0:
                 make_table(q_tables[b][:], cos_sb[b][:, 0:1, :], sin_sb[b][:, 0:1, :], q_gain)
 
+        def order_words(b, c):
+            ordered = order_pool.tile([P, ROUND_SLOTS, HID // 2], F32, name="ordered")
+            ordered_words[(b, c)] = ordered
+            for j in range(ROUND_SLOTS):
+                nc.vector.tensor_copy(
+                    out=ordered[:, j, :].rearrange("p (g u r) -> p g r u", g=PASSES, u=2),
+                    in_=x_tiles[(b, c)][:, j, :].bitcast(F32).rearrange("p (g r u) -> p g r u", g=PASSES, u=2),
+                )
+
         def transpose_slot(b, c, j):
-            words = x_tiles[(b, c)][:, j, :].bitcast(F32)
             banks = []
             for first_pass in range(0, PASSES, 2):
                 bank = banks_pool.tile([P, 2, 2, P], F32, name="bank")
                 for i in range(2):
                     start = (first_pass + i) * PASS_WORDS
                     for u in range(2):
-                        nc.tensor.transpose(bank[:, i, u, :], words[:, start + u : start + PASS_WORDS : 2], identity[:])
+                        if (b, c) in ordered_words:
+                            words = ordered_words[(b, c)][:, j, start + u * P : start + (u + 1) * P]
+                        else:
+                            words = x_tiles[(b, c)][:, j, :].bitcast(F32)[:, start + u : start + PASS_WORDS : 2]
+                        nc.tensor.transpose(bank[:, i, u, :], words, identity[:])
                 banks.append(bank)
             return banks
 
@@ -392,6 +407,8 @@ def tile_dflashattention_pa_kernel(
                 if last:
                     store_queries(n, finish_query(n, project(b, 0, 0, wq[c])))
                 key_units(n)
+                if n + ORDER_AHEAD < len(rounds):
+                    order_words(rounds[n + ORDER_AHEAD][0], rounds[n + ORDER_AHEAD][1])
                 if not last:
                     q_acc = project(b, 0, 0, wq[c])
             if n > 0:

@@ -74,6 +74,7 @@ def tile_dflashattention_pa_kernel(
         table_pool = ctx.enter_context(tc.tile_pool(name="table_pool", bufs=3))
         stage = ctx.enter_context(tc.tile_pool(name="stage", bufs=3))
         small = ctx.enter_context(tc.tile_pool(name="small", bufs=4))
+        scratch = ctx.enter_context(tc.tile_pool(name="scratch", bufs=2))
         work = ctx.enter_context(tc.tile_pool(name="work", bufs=2))
         done = ctx.enter_context(tc.tile_pool(name="done", bufs=3))
         banks_pool = ctx.enter_context(tc.psum_pool(name="banks_pool", bufs=8))
@@ -112,7 +113,6 @@ def tile_dflashattention_pa_kernel(
         identity = keep.tile([P, P], F32, name="identity")
         eps = keep.tile([P, 1], F32, name="eps")
         table_warmer = keep.tile([P, 1], F32, name="table_warmer")
-        squares = keep.tile([P, HEAD_DIM], F32, name="squares")
         idle_rows = keep.tile([P, UNIT_COLS], BF16, name="idle_rows")
 
         nc.vector.memset(ones[:], 1.0)
@@ -275,10 +275,11 @@ def tile_dflashattention_pa_kernel(
         def inverse_rms(accs):
             count = len(accs) * UNIT_HEADS
             sum_squares = small.tile([P, count], F32, name="sum_squares")
+            squares = scratch.tile([P, ROUND_SLOTS * UNIT_HEADS, HEAD_DIM], F32, name="squares")
             for i in range(len(accs)):
                 for h in range(UNIT_HEADS):
                     nc.scalar.activation(
-                        out=squares[:],
+                        out=squares[:, i * UNIT_HEADS + h, :],
                         in_=accs[i][:, h * HEAD_DIM : (h + 1) * HEAD_DIM],
                         func=ACT.Square,
                         accum_out=sum_squares[:, i * UNIT_HEADS + h : i * UNIT_HEADS + h + 1],

@@ -220,11 +220,16 @@ def tile_dflashattention_pa_kernel(
         def order_words(b, c):
             ordered = order_pool.tile([P, ROUND_SLOTS, HID // 2], F32, name="ordered")
             ordered_words[(b, c)] = ordered
-            for j in range(ROUND_SLOTS):
-                nc.vector.tensor_copy(
-                    out=ordered[:, j, :].rearrange("p (g u r) -> p g r u", g=PASSES, u=2),
-                    in_=x_tiles[(b, c)][:, j, :].bitcast(F32).rearrange("p (g r u) -> p g r u", g=PASSES, u=2),
-                )
+            nc.vector.tensor_copy(
+                out=ordered[:, 0, :].rearrange("p (g u r) -> p g r u", g=PASSES, u=2),
+                in_=x_tiles[(b, c)][:, 0, :].bitcast(F32).rearrange("p (g r u) -> p g r u", g=PASSES, u=2),
+            )
+
+        def order_second_slot(b, c):
+            nc.scalar.copy(
+                out=ordered_words[(b, c)][:, 1, :].rearrange("p (g u r) -> p g r u", g=PASSES, u=2),
+                in_=x_tiles[(b, c)][:, 1, :].bitcast(F32).rearrange("p (g r u) -> p g r u", g=PASSES, u=2),
+            )
 
         def transpose_slot(b, c, j):
             banks = []
@@ -420,3 +425,5 @@ def tile_dflashattention_pa_kernel(
                 finish_values(n - 1, v_accs)
             if n < len(rounds) - 1:
                 store_queries(n, queries)
+            if n + ORDER_AHEAD < len(rounds):
+                order_second_slot(rounds[n + ORDER_AHEAD][0], rounds[n + ORDER_AHEAD][1])

@@ -39,6 +39,27 @@ FIRST_PIECES = 2
 ORDER_AHEAD = 2
 LOADS_AHEAD = 3
 
+WK_PARTS = 2
+LOADS = "x0s0a x0s0b x0s1 wkS wkW gains new wv x1 wq ctx0 x2"
+X_BUFS = 5
+ORDER_BUFS = 2
+ORDER_FROM = 2
+WQ_AT = {3: 1, 5: 2, 7: 3}
+HEAD = "kb4 T0 kb2 T1 kb2 G0a G0bv qz0 G1a G1bv qz1 K0 gains K1 keepg tab qtab"
+
+
+def body(text):
+    out = []
+    for w in text.split():
+        parts = w.split("@")
+        out.append((parts[0], int(parts[1]) if len(parts) == 2 else 0))
+    return out
+
+
+BODY = body("L@3 K0 K1 T0@1 T1@1 sqK0 sqK1 rK0 G0a@1 rK1 G0b@1 stK0 stK1 qz0@1 G1a@1 G1b@1 qz1@1 roK sK tab@1 Q V0 V1 o0@2 sqQ cV0 rQ stQ cV1 sV roQ sQ o1s@2")
+FIRST_BODY = body("L@3 V0 V1 sqK0 sqK1 rK0 rK1 stK0 stK1 T0@1 T1@1 cV0 G0a@1 G0b@1 cV1 sV qz0@1 G1a@1 G1b@1 qz1@1 roK sK tab@1 Q o0@2 sqQ rQ stQ roQ sQ o1s@2")
+PRE_BODY = body("L@3 K0 K1 T0@1 T1@1 sqK0 sqK1 rK0 G0a@1 rK1 G0b@1 stK0 stK1 qz0@1 G1a@1 G1b@1 qz1@1 roK sK tab@1 Q V0 o0@2 sqQ cV0 sV0 rQ stQ roQ o1s@2")
+LAST_BODY = body("Q sqQ rQ stQ roQ K0 K1 sqK0 rK0 stK0 sqK1 rK1 stK1 roK0 roK1 V1@-1 cV1@-1 V0 V1 cV0 cV1 sQ@-1 sV1@-1 sQ sV0 sK0 sV1 sK1")
 FLOPS = 2 * HID * BATCH * ((CTX + Q_LEN) * 2 * KV_HEADS * HEAD_DIM + Q_LEN * Q_HEADS * HEAD_DIM)
 
 
@@ -65,12 +86,18 @@ def tile_dflashattention_pa_kernel(
     out_2,
 ):
     nc = tc.nc
-    rounds = [(b, c) for b in range(BATCH) for c in range(ROUNDS)]
+    rounds = [((0, 0), (1, 0))]
+    for b in range(BATCH):
+        for s in range(1, CTX_SLOTS, ROUND_SLOTS):
+            rounds.append(((b, s), (b, s + 1)))
+        if b == 0:
+            rounds.append(((0, CTX_SLOTS), (1, CTX_SLOTS)))
+    last_round = len(rounds) - 1
 
     with ExitStack() as ctx:
         keep = ctx.enter_context(tc.tile_pool(name="keep", bufs=1))
-        x_pool = ctx.enter_context(tc.tile_pool(name="x_pool", bufs=LOADS_AHEAD + 2))
-        order_pool = ctx.enter_context(tc.tile_pool(name="order_pool", bufs=2))
+        x_pool = ctx.enter_context(tc.tile_pool(name="x_pool", bufs=X_BUFS))
+        order_pool = ctx.enter_context(tc.tile_pool(name="order_pool", bufs=ORDER_BUFS))
         table_pool = ctx.enter_context(tc.tile_pool(name="table_pool", bufs=3))
         stage = ctx.enter_context(tc.tile_pool(name="stage", bufs=3))
         small = ctx.enter_context(tc.tile_pool(name="small", bufs=4))
@@ -80,21 +107,16 @@ def tile_dflashattention_pa_kernel(
         banks_pool = ctx.enter_context(tc.psum_pool(name="banks_pool", bufs=8))
         ctx.enter_context(tc.manual_schedule())
 
-        x_tiles = {}
-        ordered_words = {}
-        k_tables = {}
-        x_codes = {}
-        x_scales = {}
-        for b, c in rounds:
-            x_codes[(b, c)] = keep.tile(
-                [P, ROUND_SLOTS, PASSES * P], U32, name="x_codes_%d_%d" % (b, c), align_bytes=64
-            )
-            x_scales[(b, c)] = keep.tile(
-                [P, ROUND_SLOTS, PASSES * P], U8, name="x_scales_%d_%d" % (b, c), align_bytes=64
-            )
-        q_tables = [keep.tile([P, 1, 2, HEAD_DIM], F32, name="q_table_%d" % b) for b in range(BATCH)]
-        cos_sb = [keep.tile([P, SLOTS, HEAD_DIM], BF16, name="cos_%d" % b) for b in range(BATCH)]
-        sin_sb = [keep.tile([P, SLOTS, HEAD_DIM], BF16, name="sin_%d" % b) for b in range(BATCH)]
+        x_codes = []
+        x_scales = []
+        for n in range(len(rounds)):
+            x_codes.append(keep.tile([P, ROUND_SLOTS, PASSES * P], U32, name="x_codes_%d" % n, align_bytes=64))
+            x_scales.append(keep.tile([P, ROUND_SLOTS, PASSES * P], U8, name="x_scales_%d" % n, align_bytes=64))
+        q_table = keep.tile([P, BATCH, 2, HEAD_DIM], F32, name="q_table")
+        new_cos = keep.tile([P, BATCH, HEAD_DIM], BF16, name="new_cos")
+        new_sin = keep.tile([P, BATCH, HEAD_DIM], BF16, name="new_sin")
+        context_cos = [keep.tile([P, CTX_SLOTS, HEAD_DIM], BF16, name="context_cos_%d" % b) for b in range(BATCH)]
+        context_sin = [keep.tile([P, CTX_SLOTS, HEAD_DIM], BF16, name="context_sin_%d" % b) for b in range(BATCH)]
 
         def weight_tiles(name):
             words_sb = keep.tile([P, PASSES, 2 * UNIT_COLS], U8, name=name + "_words", align_bytes=64)
@@ -103,7 +125,7 @@ def tile_dflashattention_pa_kernel(
 
         wk = weight_tiles("wk")
         wv = weight_tiles("wv")
-        wq = [weight_tiles("wq%d" % c) for c in range(ROUNDS)]
+        wq = [weight_tiles("wq%d" % c) for c in range(4)]
         gain_rows = keep.tile([P, 2 * HEAD_DIM], BF16, name="gain_rows")
         ones = keep.tile([P, P], BF16, name="ones")
         gains = keep.tile([P, 2 * HEAD_DIM], F32, name="gains")
@@ -119,27 +141,32 @@ def tile_dflashattention_pa_kernel(
         nc.vector.memset(idle_rows[:], 0.0)
         nc.vector.memset(gain_rows[:], 0.0)
         nc.vector.memset(eps[:], EPS)
-        for words_sb, plane in [wk, wq[0], wv] + wq[1:]:
+        for words_sb, plane in [wk, wv] + wq:
             nc.vector.memset(plane[:].bitcast(I32), 0)
         make_identity(nc, identity[:])
         nc.scalar.activation(out=table_warmer[:], in_=eps[:], func=ACT.Abs_reciprocal_sqrt)
 
-        def load_x(b, c):
-            x_tile = x_pool.tile([P, ROUND_SLOTS, HID], BF16, name="x")
-            x_tiles[(b, c)] = x_tile
-            context = context_rows(target_hidden[b])
-            if c == 0:
-                pieces = FIRST_PIECES if b == 0 else 1
-                width = HID // pieces
-                for rows, j in ((hidden_states[b], 0), (context[:, 0, :], 1)):
-                    for i in range(pieces):
-                        columns = slice(i * width, (i + 1) * width)
-                        nc.sync.dma_start(out=x_tile[:, j, columns], in_=rows[:, columns])
-            else:
-                first = ROUND_SLOTS * c - 1
-                nc.sync.dma_start(out=x_tile[:], in_=context[:, first : first + ROUND_SLOTS, :])
+        x_tiles = {}
+        ordered_words = {}
 
-        def load_weight(tiles, words, scales, first_column):
+        def load_x(n):
+            x_tile = x_pool.tile([P, ROUND_SLOTS, HID], BF16, name="x")
+            x_tiles[n] = x_tile
+            if n == 0:
+                width = HID // FIRST_PIECES
+                for j in range(ROUND_SLOTS):
+                    for i in range(FIRST_PIECES):
+                        columns = slice(i * width, (i + 1) * width)
+                        nc.sync.dma_start(out=x_tile[:, j, columns], in_=hidden_states[j, :, columns])
+                return
+            (b0, s0), (b1, s1) = rounds[n]
+            if b0 == b1:
+                nc.sync.dma_start(out=x_tile[:], in_=context_rows(target_hidden[b0])[:, s0 - 1 : s1, :])
+            else:
+                for j, (b, s) in enumerate(rounds[n]):
+                    nc.sync.dma_start(out=x_tile[:, j, :], in_=context_rows(target_hidden[b])[:, s - 1, :])
+
+        def load_weight(tiles, words, scales, first_column, parts=1):
             words_sb, plane = tiles
             first = first_column // 4
             for r in range(4):
@@ -148,43 +175,77 @@ def tile_dflashattention_pa_kernel(
                     in_=scales.bitcast(I32)[:, r:16:4, first : first + UNIT_COLS // 4].rearrange("g q n -> q g n"),
                 )
             first = first_column // 2
-            nc.sync.dma_start(
-                out=words_sb[:].bitcast(I32),
-                in_=words.bitcast(I32)[:, :, first : first + UNIT_COLS // 2].rearrange("g p n -> p g n"),
-            )
+            for g in range(0, PASSES, PASSES // parts):
+                gs = slice(g, g + PASSES // parts)
+                nc.sync.dma_start(
+                    out=words_sb[:, gs, :].bitcast(I32),
+                    in_=words.bitcast(I32)[gs, :, first : first + UNIT_COLS // 2].rearrange("g p n -> p g n"),
+                )
 
         def load_query_weight(c):
             load_weight(wq[c], Wq_words, Wq_scales, c * UNIT_COLS)
 
-        def load_first_angles(b):
-            for table_sb, table in ((cos_sb[b], cos), (sin_sb[b], sin)):
-                nc.sync.dma_start(out=table_sb[:, 0, :], in_=table[b, CTX : CTX + Q_LEN, :])
-                nc.sync.dma_start(out=table_sb[:, 1, :], in_=context_rows(table[b, 0:CTX, :])[:, 0, :])
+        def load_new_angles():
+            for table_sb, table in ((new_cos, cos), (new_sin, sin)):
+                nc.sync.dma_start(out=table_sb[:], in_=table[:, CTX : CTX + Q_LEN, :].rearrange("b p d -> p b d"))
 
-        def load_other_angles(b):
-            for table_sb, table in ((cos_sb[b], cos), (sin_sb[b], sin)):
-                nc.sync.dma_start(out=table_sb[:, 2:SLOTS, :], in_=context_rows(table[b, 0:CTX, :])[:, 1:CTX_SLOTS, :])
+        def load_context_angles(b):
+            for table_sb, table in ((context_cos[b], cos), (context_sin[b], sin)):
+                nc.sync.dma_start(out=table_sb[:], in_=context_rows(table[b, 0:CTX, :]))
 
-        def load_round(b, c):
-            if c == 0:
-                load_first_angles(b)
-                load_other_angles(b)
-            load_x(b, c)
-            if b == 0:
-                load_query_weight(c)
+        def load_ahead(n):
+            if n < len(rounds):
+                load_x(n)
+            if n == 4:
+                load_context_angles(1)
+            if n in WQ_AT:
+                load_query_weight(WQ_AT[n])
 
-        load_x(0, 0)
-        nc.sync.dma_start(out=gain_rows[0:1, 0:HEAD_DIM], in_=k_norm_w.unsqueeze(0))
-        nc.sync.dma_start(out=gain_rows[0:1, HEAD_DIM : 2 * HEAD_DIM], in_=q_norm_w.unsqueeze(0))
-        load_weight(wk, Wk_words, Wk_scales, 0)
-        load_first_angles(0)
-        load_x(0, 1)
-        load_other_angles(0)
-        load_query_weight(0)
-        load_x(0, 2)
-        load_weight(wv, Wv_words, Wv_scales, 0)
-        load_query_weight(1)
-        load_query_weight(2)
+        for s in LOADS.split():
+            if s[0] == "x":
+                if len(s) == 2:
+                    load_x(int(s[1]))
+                else:
+                    n, j = int(s[1]), int(s[3])
+                    if n not in x_tiles:
+                        t = x_pool.tile([P, ROUND_SLOTS, HID], BF16, name="x")
+                        x_tiles[n] = t
+                    b, sl = rounds[n][j]
+                    cols = slice(0, HID) if len(s) == 4 else slice(1024 * "ab".index(s[4]), 1024 * "ab".index(s[4]) + 1024)
+                    rows = hidden_states[j, :, :] if n == 0 else context_rows(target_hidden[b])[:, sl - 1, :]
+                    nc.sync.dma_start(out=x_tiles[n][:, j, cols], in_=rows[:, cols])
+            elif s == "gains":
+                nc.sync.dma_start(out=gain_rows[0:1, 0:HEAD_DIM], in_=k_norm_w.unsqueeze(0))
+                nc.sync.dma_start(out=gain_rows[0:1, HEAD_DIM : 2 * HEAD_DIM], in_=q_norm_w.unsqueeze(0))
+            elif s == "wk":
+                load_weight(wk, Wk_words, Wk_scales, 0, WK_PARTS)
+            elif s == "wkS":
+                for r in range(4):
+                    nc.sync.dma_start(
+                        out=wk[1][r:P:32, :, :].bitcast(I32),
+                        in_=Wk_scales.bitcast(I32)[:, r:16:4, :].rearrange("g q n -> q g n"),
+                    )
+            elif s[:3] == "wkW":
+                gs = slice(0, 4) if len(s) == 3 else slice(2 * int(s[3]), 2 * int(s[3]) + 2)
+                nc.sync.dma_start(out=wk[0][:, gs, :].bitcast(I32), in_=Wk_words.bitcast(I32)[gs, :, :].rearrange("g p n -> p g n"))
+            elif s == "wv":
+                load_weight(wv, Wv_words, Wv_scales, 0)
+            elif s == "wqS":
+                for r in range(4):
+                    nc.sync.dma_start(
+                        out=wq[0][1][r:P:32, :, :].bitcast(I32),
+                        in_=Wq_scales.bitcast(I32)[:, r:16:4, 0:128].rearrange("g q n -> q g n"),
+                    )
+            elif s == "new":
+                load_new_angles()
+            elif s == "ctx0":
+                load_context_angles(0)
+            elif s == "ctx1":
+                load_context_angles(1)
+            elif s == "wq":
+                load_query_weight(0)
+            else:
+                raise ValueError(s)
 
         def spread_gains():
             bank = banks_pool.tile([P, UNIT_COLS], F32, name="bank")
@@ -208,68 +269,74 @@ def tile_dflashattention_pa_kernel(
             nc.gpsimd.tensor_tensor(out=table[:, :, 1, low], in0=sin_rows[:, :, high], in1=spread(gain[:, low]), op=ALU.mult)
             nc.gpsimd.tensor_tensor(out=table[:, :, 1, high], in0=sin_rows[:, :, low], in1=spread(minus_gain[:, high]), op=ALU.mult)
 
-        def make_tables(b, c):
-            first = ROUND_SLOTS * c
-            slots = slice(first, first + ROUND_SLOTS)
-            k_table = table_pool.tile([P, ROUND_SLOTS, 2, HEAD_DIM], F32, name="k_table")
-            k_tables[(b, c)] = k_table
-            make_table(k_table[:], cos_sb[b][:, slots, :], sin_sb[b][:, slots, :], k_gain)
-            if c == 0:
-                make_table(q_tables[b][:], cos_sb[b][:, 0:1, :], sin_sb[b][:, 0:1, :], q_gain)
+        k_tables = {}
 
-        def order_words(b, c):
-            ordered = order_pool.tile([P, ROUND_SLOTS, HID // 2], F32, name="ordered")
-            ordered_words[(b, c)] = ordered
-            nc.vector.tensor_copy(
-                out=ordered[:, 0, :].rearrange("p (g u r) -> p g r u", g=PASSES, u=2),
-                in_=x_tiles[(b, c)][:, 0, :].bitcast(F32).rearrange("p (g r u) -> p g r u", g=PASSES, u=2),
+        def make_key_table(n):
+            table = table_pool.tile([P, ROUND_SLOTS, 2, HEAD_DIM], F32, name="k_table")
+            k_tables[n] = table
+            if n == 0:
+                make_table(table[:], new_cos[:], new_sin[:], k_gain)
+                return
+            (b0, s0), (b1, s1) = rounds[n]
+            if b0 == b1:
+                slots = slice(s0 - 1, s1)
+                make_table(table[:], context_cos[b0][:, slots, :], context_sin[b0][:, slots, :], k_gain)
+            else:
+                for j, (b, s) in enumerate(rounds[n]):
+                    slots = slice(s - 1, s)
+                    make_table(table[:, j : j + 1], context_cos[b][:, slots, :], context_sin[b][:, slots, :], k_gain)
+
+        def order_words(n, j, copy):
+            if n not in ordered_words:
+                ordered = order_pool.tile([P, ROUND_SLOTS, HID // 2], F32, name="ordered")
+                ordered_words[n] = ordered
+            copy(
+                out=ordered_words[n][:, j, :].rearrange("p (g u r) -> p g r u", g=PASSES, u=2),
+                in_=x_tiles[n][:, j, :].bitcast(F32).rearrange("p (g r u) -> p g r u", g=PASSES, u=2),
             )
 
-        def order_second_slot(b, c):
-            nc.scalar.copy(
-                out=ordered_words[(b, c)][:, 1, :].rearrange("p (g u r) -> p g r u", g=PASSES, u=2),
-                in_=x_tiles[(b, c)][:, 1, :].bitcast(F32).rearrange("p (g r u) -> p g r u", g=PASSES, u=2),
-            )
+        t_banks = {}
 
-        def transpose_slot(b, c, j):
-            banks = []
+        def transpose_slot(n, j):
+            t_banks[(n, j)] = []
             for first_pass in range(0, PASSES, 2):
                 bank = banks_pool.tile([P, 2, 2, P], F32, name="bank")
                 for i in range(2):
                     start = (first_pass + i) * PASS_WORDS
                     for u in range(2):
-                        if (b, c) in ordered_words:
-                            words = ordered_words[(b, c)][:, j, start + u * P : start + (u + 1) * P]
+                        if n in ordered_words:
+                            words = ordered_words[n][:, j, start + u * P : start + (u + 1) * P]
                         else:
-                            words = x_tiles[(b, c)][:, j, :].bitcast(F32)[:, start + u : start + PASS_WORDS : 2]
+                            words = x_tiles[n][:, j, :].bitcast(F32)[:, start + u : start + PASS_WORDS : 2]
                         nc.tensor.transpose(bank[:, i, u, :], words, identity[:])
-                banks.append(bank)
-            return banks
+                t_banks[(n, j)].append(bank)
 
-        def group_slot(banks):
-            grouped = stage.tile([P, PASSES * P * PACK], BF16, name="grouped", align_bytes=64)
-            grouped_words = grouped[:].bitcast(F32).rearrange("p (g r u) -> p g r u", g=PASSES, u=2)
-            for half in range(2):
-                nc.scalar.copy(
-                    out=grouped_words[:, 2 * half : 2 * half + 2, :, :],
-                    in_=banks[half][:].rearrange("p g u r -> p g r u"),
-                )
-            return grouped
+        grouped = {}
 
-        def quantise_slot(b, c, j, grouped):
-            nc.vector.quantize_mx(
-                out=x_codes[(b, c)][:, j, :].bitcast(FP8X4), scales=x_scales[(b, c)][:, j, :], in_=grouped[:]
+        def group(n, j, half, copy):
+            if half == 0:
+                g = stage.tile([P, PASSES * P * PACK], BF16, name="grouped", align_bytes=64)
+                grouped[(n, j)] = g
+            words = grouped[(n, j)][:].bitcast(F32).rearrange("p (g r u) -> p g r u", g=PASSES, u=2)
+            copy(
+                out=words[:, 2 * half : 2 * half + 2, :, :],
+                in_=t_banks[(n, j)][half][:].rearrange("p g u r -> p g r u"),
             )
 
-        def project(b, c, j, weight):
+        def quantise(n, j):
+            nc.vector.quantize_mx(
+                out=x_codes[n][:, j, :].bitcast(FP8X4), scales=x_scales[n][:, j, :], in_=grouped[(n, j)][:]
+            )
+
+        def project(n, j, weight):
             words_sb, plane = weight
             acc = banks_pool.tile([P, UNIT_COLS], F32, name="bank")
             for g in range(PASSES):
                 tokens = slice(g * P, (g + 1) * P)
                 nc.tensor.matmul_mx(
                     out=acc[:],
-                    lhsT=x_codes[(b, c)][:, j, tokens].bitcast(FP8X4),
-                    lhsT_scale=x_scales[(b, c)][:, j, tokens],
+                    lhsT=x_codes[n][:, j, tokens].bitcast(FP8X4),
+                    lhsT_scale=x_scales[n][:, j, tokens],
                     rhs=words_sb[:, g, :].bitcast(FP4X4),
                     rhs_scale=plane[:, g, :],
                     start=(g == 0),
@@ -277,23 +344,18 @@ def tile_dflashattention_pa_kernel(
                 )
             return acc
 
-        def inverse_rms(accs):
-            count = len(accs) * UNIT_HEADS
-            sum_squares = small.tile([P, count], F32, name="sum_squares")
-            squares = scratch.tile([P, ROUND_SLOTS * UNIT_HEADS, HEAD_DIM], F32, name="squares")
-            for i in range(len(accs)):
-                for h in range(UNIT_HEADS):
-                    nc.scalar.activation(
-                        out=squares[:, i * UNIT_HEADS + h, :],
-                        in_=accs[i][:, h * HEAD_DIM : (h + 1) * HEAD_DIM],
-                        func=ACT.Square,
-                        accum_out=sum_squares[:, i * UNIT_HEADS + h : i * UNIT_HEADS + h + 1],
-                    )
-            inv_rms = small.tile([P, count], F32, name="inv_rms")
-            nc.scalar.activation(
-                out=inv_rms[:], in_=sum_squares[:], func=ACT.Abs_reciprocal_sqrt, scale=1.0 / HEAD_DIM, bias=eps[:]
-            )
-            return inv_rms
+        def squares(acc, sum_squares, first):
+            unread = scratch.tile([P, UNIT_HEADS, HEAD_DIM], F32, name="squares")
+            for h in range(UNIT_HEADS):
+                nc.scalar.activation(
+                    out=unread[:, h, :],
+                    in_=acc[:, h * HEAD_DIM : (h + 1) * HEAD_DIM],
+                    func=ACT.Square,
+                    accum_out=sum_squares[:, first + h : first + h + 1],
+                )
+
+        def rsqrt(out, sums):
+            nc.scalar.activation(out=out, in_=sums, func=ACT.Abs_reciprocal_sqrt, scale=1.0 / HEAD_DIM, bias=eps[:])
 
         def norm_and_scale(acc, inv_rms, table, products):
             for h in range(UNIT_HEADS):
@@ -316,77 +378,104 @@ def tile_dflashattention_pa_kernel(
                 op=ALU.add,
             )
 
-        def store_slot(pair, out, b, c, j):
-            slot = ROUND_SLOTS * c + j
-            if slot == 0:
+        def store_slot(tile, out, n, j):
+            b, s = rounds[n][j]
+            if s == 0:
                 rows = out[b, :, CTX : CTX + Q_LEN, :].rearrange("h p d -> p h d")
             else:
-                rows = out[b, :, 0:CTX, :].rearrange("h (p i) d -> p h i d", i=CTX_SLOTS)[:, :, slot - 1, :]
-            nc.sync.dma_start(out=rows, in_=pair[:, :, j, :])
+                rows = out[b, :, 0:CTX, :].rearrange("h (p i) d -> p h i d", i=CTX_SLOTS)[:, :, s - 1, :]
+            nc.sync.dma_start(out=rows, in_=tile[:, :, j, :])
 
-        def store_pair(pair, out, b, c):
-            if c == 0:
+        def store_pair(tile, out, n):
+            (b0, s0), (b1, s1) = rounds[n]
+            if b0 != b1 :
                 for j in range(ROUND_SLOTS):
-                    store_slot(pair, out, b, c, j)
+                    store_slot(tile, out, n, j)
             else:
-                first = ROUND_SLOTS * c - 1
-                context = out[b, :, 0:CTX, :].rearrange("h (p i) d -> p h i d", i=CTX_SLOTS)
-                nc.sync.dma_start(out=context[:, :, first : first + ROUND_SLOTS, :], in_=pair)
+                context = out[b0, :, 0:CTX, :].rearrange("h (p i) d -> p h i d", i=CTX_SLOTS)
+                nc.sync.dma_start(out=context[:, :, s0 - 1 : s1, :], in_=tile)
 
-        def key_units(n):
-            b, c = rounds[n]
-            following = rounds[n + 1] if n + 1 < len(rounds) else None
-            keys = done.tile([P, KV_HEADS * ROUND_SLOTS, HEAD_DIM], F32, name="keys")
-            k_accs = [project(b, c, j, wk) for j in range(ROUND_SLOTS)]
-            if following is not None:
-                banks = [transpose_slot(following[0], following[1], j) for j in range(ROUND_SLOTS)]
-            products = work.tile([P, KV_HEADS * ROUND_SLOTS, 2, HEAD_DIM], F32, name="k_products")
-            pair = keys[:].rearrange("p (h i) d -> p h i d", i=ROUND_SLOTS)
-            slot_rows = [slice(j, KV_HEADS * ROUND_SLOTS, ROUND_SLOTS) for j in range(ROUND_SLOTS)]
-            if following is None:
-                for j in range(ROUND_SLOTS):
-                    norm_and_scale(
-                        k_accs[j], inverse_rms([k_accs[j]]), k_tables[(b, c)][:, j, :, :], products[:, slot_rows[j], :, :]
-                    )
-                    rotate(products[:, slot_rows[j], :, :], keys[:, slot_rows[j], :], nc.vector)
-                    store_slot(pair, out_1, b, c, j)
-                return
-            inv_rms = inverse_rms(k_accs)
-            grouped = [group_slot(banks[j]) for j in range(ROUND_SLOTS)]
-            for j in range(ROUND_SLOTS):
-                norm_and_scale(
-                    k_accs[j],
-                    inv_rms[:, j * UNIT_HEADS : (j + 1) * UNIT_HEADS],
-                    k_tables[(b, c)][:, j, :, :],
-                    products[:, slot_rows[j], :, :],
-                )
-                quantise_slot(following[0], following[1], j, grouped[j])
-            rotate(products, keys[:], nc.vector)
-            store_pair(pair, out_1, b, c)
-            make_tables(following[0], following[1])
+        st = {}
 
-        def finish_query(n, q_acc):
-            b, c = rounds[n]
-            queries = done.tile([P, UNIT_HEADS, HEAD_DIM], F32, name="queries")
-            products = work.tile([P, UNIT_HEADS, 2, HEAD_DIM], F32, name="q_products")
-            norm_and_scale(q_acc, inverse_rms([q_acc]), q_tables[b][:, 0, :, :], products)
-            rotate(products, queries[:], nc.gpsimd)
-            return queries
-
-        def finish_values(n, v_accs):
-            b, c = rounds[n]
-            values = done.tile([P, KV_HEADS, ROUND_SLOTS, HEAD_DIM], F32, name="values")
-            for j in range(ROUND_SLOTS):
-                nc.scalar.copy(out=values[:, :, j, :], in_=v_accs[j][:].rearrange("p (h d) -> p h d", h=KV_HEADS))
-                if n == len(rounds) - 1:
-                    store_slot(values[:], out_2, b, c, j)
-            if n < len(rounds) - 1:
-                store_pair(values[:], out_2, b, c)
-
-        def store_queries(n, queries):
-            b, c = rounds[n]
-            heads = slice(c * UNIT_HEADS, (c + 1) * UNIT_HEADS)
-            nc.sync.dma_start(out=out_0[b, heads, :, :].rearrange("h p d -> p h d"), in_=queries[:])
+        def step(name, n):
+            S = st.setdefault(n, {})
+            if name in ("K0", "K1"):
+                S[name] = project(n, int(name[1]), wk)
+            elif name in ("V0", "V1"):
+                S[name] = project(n, int(name[1]), wv)
+            elif name == "Q":
+                S["Q"] = project(0, n % 2, wq[n // 2])
+            elif name in ("T0", "T1"):
+                transpose_slot(n, int(name[1]))
+            elif name[0] == "G":
+                group(n, int(name[1]), "ab".index(name[2]), nc.vector.tensor_copy if name[3:] == "v" else nc.scalar.copy)
+            elif name in ("qz0", "qz1"):
+                quantise(n, int(name[2]))
+            elif name in ("sqK0", "sqK1"):
+                if "ssK" not in S:
+                    t = small.tile([P, 8], F32, name="sum_squares")
+                    u = small.tile([P, 8], F32, name="inv_rms")
+                    S["ssK"] = t
+                    S["inK"] = u
+                squares(S[name[2:]], S["ssK"], 4 * int(name[3]))
+            elif name in ("rK", "rK0", "rK1"):
+                c = slice(0, 8) if name == "rK" else slice(4 * int(name[2]), 4 * int(name[2]) + 4)
+                rsqrt(S["inK"][:, c], S["ssK"][:, c])
+            elif name == "sqQ":
+                t = small.tile([P, 4], F32, name="sum_squares_q")
+                u = small.tile([P, 4], F32, name="inv_rms_q")
+                S["ssQ"] = t
+                S["inQ"] = u
+                squares(S["Q"], t, 0)
+            elif name == "rQ":
+                rsqrt(S["inQ"][:], S["ssQ"][:])
+            elif name in ("stK0", "stK1"):
+                j = int(name[3])
+                if "pK" not in S:
+                    t = work.tile([P, KV_HEADS * ROUND_SLOTS, 2, HEAD_DIM], F32, name="k_products")
+                    u = done.tile([P, KV_HEADS * ROUND_SLOTS, HEAD_DIM], F32, name="keys")
+                    S["pK"] = t
+                    S["keys"] = u
+                norm_and_scale(S["K%d" % j], S["inK"][:, 4 * j : 4 * j + 4], k_tables[n][:, j, :, :], S["pK"][:, j : 8 : 2, :, :])
+            elif name in ("roK", "roK0", "roK1", "roK0g", "roK1g"):
+                r = slice(0, 8) if name == "roK" else slice(int(name[3]), 8, 2)
+                rotate(S["pK"][:, r], S["keys"][:, r], nc.gpsimd if name[-1] == "g" else nc.vector)
+            elif name in ("sK", "sK0", "sK1"):
+                pair = S["keys"][:].rearrange("p (h i) d -> p h i d", i=ROUND_SLOTS)
+                if name == "sK":
+                    store_pair(pair, out_1, n)
+                else:
+                    store_slot(pair, out_1, n, int(name[2]))
+            elif name == "stQ":
+                t = work.tile([P, UNIT_HEADS, 2, HEAD_DIM], F32, name="q_products")
+                u = done.tile([P, UNIT_HEADS, HEAD_DIM], F32, name="queries")
+                S["pQ"] = t
+                S["queries"] = u
+                norm_and_scale(S["Q"], S["inQ"], q_table[:, n % 2, :, :], t)
+            elif name in ("roQ", "roQv"):
+                rotate(S["pQ"], S["queries"][:], nc.vector if name == "roQv" else nc.gpsimd)
+            elif name == "sQ":
+                heads = slice((n // 2) * UNIT_HEADS, (n // 2 + 1) * UNIT_HEADS)
+                nc.sync.dma_start(out=out_0[n % 2, heads, :, :].rearrange("h p d -> p h d"), in_=S["queries"][:])
+            elif name in ("cV0", "cV1"):
+                j = int(name[2])
+                if "values" not in S:
+                    t = done.tile([P, KV_HEADS, ROUND_SLOTS, HEAD_DIM], F32, name="values")
+                    S["values"] = t
+                nc.scalar.copy(out=S["values"][:, :, j, :], in_=S["V%d" % j][:].rearrange("p (h d) -> p h d", h=KV_HEADS))
+            elif name in ("sV", "sV0", "sV1"):
+                if name == "sV":
+                    store_pair(S["values"][:], out_2, n)
+                else:
+                    store_slot(S["values"][:], out_2, n, int(name[2]))
+            elif name == "tab":
+                make_key_table(n)
+            elif name in ("o0", "o1", "o0s", "o1s"):
+                order_words(n, int(name[1]), nc.scalar.copy if name[2:] == "s" else nc.vector.tensor_copy)
+            elif name == "L":
+                load_ahead(n)
+            else:
+                raise ValueError(name)
 
         idle_bank = banks_pool.tile([P, UNIT_COLS], F32, name="bank")
 
@@ -394,36 +483,25 @@ def tile_dflashattention_pa_kernel(
             for i in range(count):
                 nc.tensor.matmul(out=idle_bank[:], lhsT=ones[:], rhs=idle_rows[:], start=True, stop=True)
 
-        keep_busy(4)
-        first_banks = [transpose_slot(0, 0, 0)]
-        gains_bank = spread_gains()
-        keep_busy(2)
-        first_banks.append(transpose_slot(0, 0, 1))
-        keep_busy(3)
-        quantise_slot(0, 0, 0, group_slot(first_banks[0]))
-        keep_gains(gains_bank)
-        make_tables(0, 0)
-        quantise_slot(0, 0, 1, group_slot(first_banks[1]))
-        for n in range(len(rounds) + 1):
-            if n + LOADS_AHEAD < len(rounds):
-                load_round(rounds[n + LOADS_AHEAD][0], rounds[n + LOADS_AHEAD][1])
-            last = n == len(rounds) - 1
-            if n < len(rounds):
-                b, c = rounds[n]
-                if last:
-                    store_queries(n, finish_query(n, project(b, 0, 0, wq[c])))
-                key_units(n)
-                if n + ORDER_AHEAD < len(rounds):
-                    order_words(rounds[n + ORDER_AHEAD][0], rounds[n + ORDER_AHEAD][1])
-                if not last:
-                    q_acc = project(b, 0, 0, wq[c])
-            if n > 0:
-                v_accs = [project(rounds[n - 1][0], rounds[n - 1][1], j, wv) for j in range(ROUND_SLOTS)]
-            if n < len(rounds) - 1:
-                queries = finish_query(n, q_acc)
-            if n > 0:
-                finish_values(n - 1, v_accs)
-            if n < len(rounds) - 1:
-                store_queries(n, queries)
-            if n + ORDER_AHEAD < len(rounds):
-                order_second_slot(rounds[n + ORDER_AHEAD][0], rounds[n + ORDER_AHEAD][1])
+        for s in HEAD.split():
+            if s == "gains":
+                gains_bank = spread_gains()
+            elif s == "keepg":
+                keep_gains(gains_bank)
+            elif s == "qtab":
+                make_table(q_table[:], new_cos[:], new_sin[:], q_gain)
+            elif s[:2] == "kb":
+                keep_busy(int(s[2:]))
+            else:
+                step(s, 0)
+        for n in range(len(rounds)):
+            for item in (FIRST_BODY if n == 0 else LAST_BODY if n == last_round else PRE_BODY if n == last_round - 1 else BODY):
+                name, shift = item
+                m = n + shift
+                if m < 0 or m >= len(rounds):
+                    continue
+                if name[0] == "o" and m < ORDER_FROM:
+                    continue
+                if n > last_round and shift >= 0:
+                    continue
+                step(name, m)

@@ -40,7 +40,7 @@ ORDER_AHEAD = 2
 LOADS_AHEAD = 3
 
 WK_PARTS = 2
-LOADS = "x0s0a x0s0b x0s1 wkS wkW gains new wv x1 wq ctx0 x2"
+LOADS = "x0s0a x0s0b x0s1 wkS wkW gains wvW new wvS x1s0 x1s1 wqW wqS ctx0 x2"
 X_BUFS = 5
 ORDER_BUFS = 2
 ORDER_FROM = 2
@@ -129,9 +129,10 @@ def tile_dflashattention_pa_kernel(
         gain_rows = keep.tile([P, 2 * HEAD_DIM], BF16, name="gain_rows")
         ones = keep.tile([P, P], BF16, name="ones")
         gains = keep.tile([P, 2 * HEAD_DIM], F32, name="gains")
-        minus_gains = keep.tile([P, 2 * HEAD_DIM], F32, name="minus_gains")
-        k_gain = (gains[:, 0:HEAD_DIM], minus_gains[:, 0:HEAD_DIM])
-        q_gain = (gains[:, HEAD_DIM : 2 * HEAD_DIM], minus_gains[:, HEAD_DIM : 2 * HEAD_DIM])
+        signed_gains = keep.tile([P, 2, 2, HALF], F32, name="signed_gains")
+        signed_rows = signed_gains[:].rearrange("p r s j -> p r (s j)")
+        k_gain = (gains[:, 0:HEAD_DIM], signed_rows[:, 0, :])
+        q_gain = (gains[:, HEAD_DIM : 2 * HEAD_DIM], signed_rows[:, 1, :])
         identity = keep.tile([P, P], F32, name="identity")
         eps = keep.tile([P, 1], F32, name="eps")
         table_warmer = keep.tile([P, 1], F32, name="table_warmer")
@@ -230,6 +231,16 @@ def tile_dflashattention_pa_kernel(
                 nc.sync.dma_start(out=wk[0][:, gs, :].bitcast(I32), in_=Wk_words.bitcast(I32)[gs, :, :].rearrange("g p n -> p g n"))
             elif s == "wv":
                 load_weight(wv, Wv_words, Wv_scales, 0)
+            elif s == "wvS":
+                for r in range(4):
+                    nc.sync.dma_start(
+                        out=wv[1][r:P:32, :, :].bitcast(I32),
+                        in_=Wv_scales.bitcast(I32)[:, r:16:4, :].rearrange("g q n -> q g n"),
+                    )
+            elif s == "wvW":
+                nc.sync.dma_start(out=wv[0][:].bitcast(I32), in_=Wv_words.bitcast(I32).rearrange("g p n -> p g n"))
+            elif s == "wqW":
+                nc.sync.dma_start(out=wq[0][0][:].bitcast(I32), in_=Wq_words.bitcast(I32)[:, :, 0:256].rearrange("g p n -> p g n"))
             elif s == "wqS":
                 for r in range(4):
                     nc.sync.dma_start(
@@ -254,20 +265,25 @@ def tile_dflashattention_pa_kernel(
 
         def keep_gains(bank):
             nc.scalar.copy(out=gains[:], in_=bank[:, 0 : 2 * HEAD_DIM])
-            nc.scalar.mul(out=minus_gains[:], in_=bank[:, 0 : 2 * HEAD_DIM], mul=-1.0)
+            halves = bank[:, 0 : 2 * HEAD_DIM].rearrange("p (r s j) -> p r s j", r=2, s=2)
+            nc.scalar.copy(out=signed_gains[:, :, 0, :], in_=halves[:, :, 0, :])
+            nc.scalar.mul(out=signed_gains[:, :, 1, :], in_=halves[:, :, 1, :], mul=-1.0)
 
         def make_table(table, cos_rows, sin_rows, gain):
             count = table.shape[1]
-            gain, minus_gain = gain
+            gain, signed_gain = gain
 
             def spread(columns):
-                return columns.unsqueeze(1).to_broadcast([P, count, columns.shape[1]])
+                return columns.unsqueeze(1).to_broadcast([P, count, HEAD_DIM])
 
-            low = slice(0, HALF)
-            high = slice(HALF, HEAD_DIM)
             nc.gpsimd.tensor_tensor(out=table[:, :, 0, :], in0=cos_rows, in1=spread(gain), op=ALU.mult)
-            nc.gpsimd.tensor_tensor(out=table[:, :, 1, low], in0=sin_rows[:, :, high], in1=spread(gain[:, low]), op=ALU.mult)
-            nc.gpsimd.tensor_tensor(out=table[:, :, 1, high], in0=sin_rows[:, :, low], in1=spread(minus_gain[:, high]), op=ALU.mult)
+            halves = "p r (s j) -> p r s j"
+            nc.gpsimd.tensor_tensor(
+                out=table[:, :, 1, :].rearrange(halves, s=2),
+                in0=sin_rows.rearrange(halves, s=2)[:, :, ::-1, :],
+                in1=spread(signed_gain).rearrange(halves, s=2),
+                op=ALU.mult,
+            )
 
         k_tables = {}
 

@@ -56,7 +56,7 @@ def body(text):
     return out
 
 
-BODY = body("L@3 K0 K1 T0@1 T1@1 sqK0 sqK1 rK0 G0a@1 rK1 G0b@1 stK0 stK1 qz0@1 G1a@1 G1b@1 qz1@1 roK sK tab@1 Q V0 V1 o0@2 sqQ cV0 rQ stQ cV1 sV roQ sQ o1s@2")
+BODY = body("L@3 K0 K1 T0@1 V0 T1@1 sqK0 sqK1 rK0 G0a@1 rK1 G0b@1 stK0 stK1 qz0@1 cV0 G1a@1 G1b@1 qz1@1 roK sK tab@1 Q V1 o0@2 sqQ rQ stQ cV1 sV roQ sQ o1s@2")
 FIRST_BODY = body("L@3 V0 V1 sqK0 sqK1 rK0 rK1 stK0 stK1 T0@1 T1@1 cV0 G0a@1 G0b@1 cV1 sV qz0@1 G1a@1 G1b@1 qz1@1 roK sK tab@1 Q o0@2 sqQ rQ stQ roQ sQ o1s@2")
 PRE_BODY = body("L@3 K0 K1 T0@1 T1@1 sqK0 sqK1 rK0 G0a@1 rK1 G0b@1 stK0 stK1 qz0@1 G1a@1 G1b@1 qz1@1 roK sK tab@1 Q V0 o0@2 sqQ cV0 sV0 rQ stQ roQ o1s@2")
 LAST_BODY = body("Q sqQ rQ stQ roQ K0 K1 sqK0 rK0 stK0 sqK1 rK1 stK1 roK0 roK1 V1@-1 cV1@-1 V0 V1 cV0 cV1 sQ@-1 sV1@-1 sQ sV0 sK0 sV1 sK1")

@@ -57,8 +57,8 @@ def body(text):
 
 
 BODY = body("L@3 K0 K1 T0@1 V0 T1@1 sqK0 sqK1 rK0 G0a@1 rK1 G0b@1 stK0 stK1 qz0@1 cV0 G1a@1 G1b@1 qz1@1 roK sK tab@1 Q V1 o0@2 sqQ rQ stQ cV1 sV roQ sQ o1s@2")
-FIRST_BODY = body("L@3 V0 V1 sqK0 sqK1 rK0 rK1 stK0 stK1 T0@1 T1@1 cV0 G0a@1 G0b@1 cV1 sV qz0@1 G1a@1 G1b@1 qz1@1 roK sK tab@1 Q o0@2 sqQ rQ stQ roQ sQ o1s@2")
-PRE_BODY = body("L@3 K0 K1 T0@1 T1@1 sqK0 sqK1 rK0 G0a@1 rK1 G0b@1 stK0 stK1 qz0@1 G1a@1 G1b@1 qz1@1 roK sK tab@1 Q V0 o0@2 sqQ cV0 sV0 rQ stQ roQ o1s@2")
+FIRST_BODY = body("L@3 V0 sqK0 sqK1 rK0 rK1 stK0 stK1 T0@1 cV0 V1 G0a@1 G0b@1 T1@1 qz0@1 cV1 sV G1a@1 G1b@1 qz1@1 roK sK tab@1 Q o0@2 sqQ rQ stQ roQ sQ o1s@2")
+PRE_BODY = body("L@3 K0 K1 T0@1 V0 T1@1 sqK0 sqK1 rK0 G0a@1 rK1 G0b@1 stK0 stK1 qz0@1 cV0 sV0 G1a@1 G1b@1 qz1@1 roK sK tab@1 Q o0@2 sqQ rQ stQ roQ o1s@2")
 LAST_BODY = body("Q sqQ rQ stQ roQ K0 K1 sqK0 rK0 stK0 sqK1 rK1 stK1 roK0 roK1 V1@-1 cV1@-1 V0 V1 cV0 cV1 sQ@-1 sV1@-1 sQ sV0 sK0 sV1 sK1")
 FLOPS = 2 * HID * BATCH * ((CTX + Q_LEN) * 2 * KV_HEADS * HEAD_DIM + Q_LEN * Q_HEADS * HEAD_DIM)
 
@@ -453,8 +453,8 @@ def tile_dflashattention_pa_kernel(
                     S["pK"] = t
                     S["keys"] = u
                 norm_and_scale(S["K%d" % j], S["inK"][:, 4 * j : 4 * j + 4], k_tables[n][:, j, :, :], S["pK"][:, j : 8 : 2, :, :])
-            elif name in ("roK", "roK0", "roK1", "roK0g", "roK1g"):
-                r = slice(0, 8) if name == "roK" else slice(int(name[3]), 8, 2)
+            elif name in ("roK", "roKg", "roK0", "roK1", "roK0g", "roK1g"):
+                r = slice(0, 8) if name in ("roK", "roKg") else slice(int(name[3]), 8, 2)
                 rotate(S["pK"][:, r], S["keys"][:, r], nc.gpsimd if name[-1] == "g" else nc.vector)
             elif name in ("sK", "sK0", "sK1"):
                 pair = S["keys"][:].rearrange("p (h i) d -> p h i d", i=ROUND_SLOTS)

@@ -56,9 +56,9 @@ def body(text):
     return out
 
 
-BODY = body("L@3 K0 K1 T0@1 V0 T1@1 sqK0 sqK1 rK0 G0a@1 rK1 G0b@1 stK0 stK1 qz0@1 cV0 G1a@1 G1b@1 qz1@1 roK sK tab@1 Q V1 o0@2 sqQ rQ stQ cV1 sV roQ sQ o1s@2")
-FIRST_BODY = body("L@3 V0 sqK0 sqK1 rK0 rK1 stK0 stK1 T0@1 cV0 V1 G0a@1 G0b@1 T1@1 qz0@1 cV1 sV G1a@1 G1b@1 qz1@1 roK sK tab@1 Q o0@2 sqQ rQ stQ roQ sQ o1s@2")
-PRE_BODY = body("L@3 K0 K1 T0@1 V0 T1@1 sqK0 sqK1 rK0 G0a@1 rK1 G0b@1 stK0 stK1 qz0@1 cV0 sV0 G1a@1 G1b@1 qz1@1 roK sK tab@1 Q o0@2 sqQ rQ stQ roQ o1s@2")
+BODY = body("L@3 K0 K1 T0@1 V0 T1@1 sqK0 sqK1 rK0 G0a@1 rK1 G0b@1 stK0 stK1 qz0@1 cV0 G1a@1 G1b@1 qz1@1 roK sK tab@1 Q V1 sqQ rQ stQ cV1 sV roQ sQ o1s@2")
+FIRST_BODY = body("L@3 V0 sqK0 sqK1 rK0 rK1 stK0 stK1 T0@1 cV0 V1 G0a@1 G0b@1 T1@1 qz0@1 cV1 sV G1a@1 G1b@1 qz1@1 roK sK tab@1 Q sqQ rQ stQ roQ sQ o1s@2")
+PRE_BODY = body("L@3 K0 K1 T0@1 V0 T1@1 sqK0 sqK1 rK0 G0a@1 rK1 G0b@1 stK0 stK1 qz0@1 cV0 sV0 G1a@1 G1b@1 qz1@1 roK sK tab@1 Q sqQ rQ stQ roQ o1s@2")
 LAST_BODY = body("Q sqQ rQ stQ roQ K0 K1 sqK0 rK0 stK0 sqK1 rK1 stK1 roK0 roK1 V1@-1 cV1@-1 V0 V1 cV0 cV1 sQ@-1 sV1@-1 sQ sV0 sK0 sV1 sK1")
 FLOPS = 2 * HID * BATCH * ((CTX + Q_LEN) * 2 * KV_HEADS * HEAD_DIM + Q_LEN * Q_HEADS * HEAD_DIM)
 
@@ -303,11 +303,10 @@ def tile_dflashattention_pa_kernel(
                     make_table(table[:, j : j + 1], context_cos[b][:, slots, :], context_sin[b][:, slots, :], k_gain)
 
         def order_words(n, j, copy):
-            if n not in ordered_words:
-                ordered = order_pool.tile([P, ROUND_SLOTS, HID // 2], F32, name="ordered")
-                ordered_words[n] = ordered
+            ordered = order_pool.tile([P, HID // 2], F32, name="ordered")
+            ordered_words[(n, j)] = ordered
             copy(
-                out=ordered_words[n][:, j, :].rearrange("p (g u r) -> p g r u", g=PASSES, u=2),
+                out=ordered[:].rearrange("p (g u r) -> p g r u", g=PASSES, u=2),
                 in_=x_tiles[n][:, j, :].bitcast(F32).rearrange("p (g r u) -> p g r u", g=PASSES, u=2),
             )
 
@@ -320,8 +319,8 @@ def tile_dflashattention_pa_kernel(
                 for i in range(2):
                     start = (first_pass + i) * PASS_WORDS
                     for u in range(2):
-                        if n in ordered_words:
-                            words = ordered_words[n][:, j, start + u * P : start + (u + 1) * P]
+                        if (n, j) in ordered_words:
+                            words = ordered_words[(n, j)][:, start + u * P : start + (u + 1) * P]
                         else:
                             words = x_tiles[n][:, j, :].bitcast(F32)[:, start + u : start + PASS_WORDS : 2]
                         nc.tensor.transpose(bank[:, i, u, :], words, identity[:])

@@ -43,7 +43,7 @@ WK_PARTS = 2
 LOADS = "x0s0a x0s0b x0s1 wkS wkW gains wvW new wvS x1s0 x1s1 wqW wqS ctx0 x2"
 X_BUFS = 5
 ORDER_BUFS = 2
-ORDER_FROM = 2
+ORDER_FROM = 9
 WQ_AT = {3: 1, 5: 2, 7: 3}
 HEAD = "kb4 T0 kb2 T1 kb2 G0a G0bv qz0 G1a G1bv qz1 K0 gains K1 keepg tab qtab"
 
@@ -56,9 +56,10 @@ def body(text):
     return out
 
 
-BODY = body("L@3 K0 K1 T0@1 V0 T1@1 sqK0 sqK1 rK0 G0a@1 rK1 G0b@1 stK0 stK1 qz0@1 cV0 G1a@1 G1b@1 qz1@1 roK sK tab@1 Q V1 sqQ rQ stQ cV1 sV roQ sQ o1s@2")
-FIRST_BODY = body("L@3 V0 sqK0 sqK1 rK0 rK1 stK0 stK1 T0@1 cV0 V1 G0a@1 G0b@1 T1@1 qz0@1 cV1 sV G1a@1 G1b@1 qz1@1 roK sK tab@1 Q sqQ rQ stQ roQ sQ o1s@2")
-PRE_BODY = body("L@3 K0 K1 T0@1 V0 T1@1 sqK0 sqK1 rK0 G0a@1 rK1 G0b@1 stK0 stK1 qz0@1 cV0 sV0 G1a@1 G1b@1 qz1@1 roK sK tab@1 Q sqQ rQ stQ roQ o1s@2")
+BODY = body("L@3 K0 K1 T0@1 V0 T1@1 sqK0 sqK1 rK0 G0a@1 rK1 G0b@1 stK0 stK1 qz0@1 cV0 G1a@1 G1b@1 qz1@1 roK sK tab@1 Q V1 sqQ rQ stQ cV1 sV roQ sQ")
+FIRST_BODY = body("L@3 V0 sqK0 sqK1 rK0 rK1 stK0 stK1 T0@1 cV0 V1 G0a@1 G0b@1 T1@1 qz0@1 cV1 sV G1a@1 G1b@1 qz1@1 roK sK tab@1 Q sqQ rQ stQ roQ sQ")
+PRE_BODY = body("L@3 K0 K1 T0@1 V0 T1@1 sqK0 sqK1 rK0 G0a@1 rK1 G0b@1 stK0 stK1 qz0@1 cV0 sV0 G1a@1 G1b@1 qz1@1 roK sK tab@1 Q sqQ rQ stQ roQ")
+PRE2_BODY = body("L@3 K0 K1 T0@1 V0 T1@1 sqK0 sqK1 rK0 G0a@1 rK1 G0b@1 stK0 stK1 qz0@1 cV0 G1a@1 G1b@1 qz1@1 roK sK tab@1 Q V1 sqQ rQ stQ cV1 sV roQ sQ")
 LAST_BODY = body("Q sqQ rQ stQ roQ K0 K1 sqK0 rK0 stK0 sqK1 rK1 stK1 roK0 roK1 V1@-1 cV1@-1 V0 V1 cV0 cV1 sQ@-1 sV1@-1 sQ sV0 sK0 sV1 sK1")
 FLOPS = 2 * HID * BATCH * ((CTX + Q_LEN) * 2 * KV_HEADS * HEAD_DIM + Q_LEN * Q_HEADS * HEAD_DIM)
 
@@ -510,7 +511,7 @@ def tile_dflashattention_pa_kernel(
             else:
                 step(s, 0)
         for n in range(len(rounds)):
-            for item in (FIRST_BODY if n == 0 else LAST_BODY if n == last_round else PRE_BODY if n == last_round - 1 else BODY):
+            for item in (FIRST_BODY if n == 0 else LAST_BODY if n == last_round else PRE_BODY if n == last_round - 1 else PRE2_BODY if n == last_round - 2 else BODY):
                 name, shift = item
                 m = n + shift
                 if m < 0 or m >= len(rounds):

@@ -43,7 +43,7 @@ WK_PARTS = 2
 LOADS = "x0s0a x0s0b x0s1 wkS wkW gains wvW new wvS x1s0 x1s1 wqW wqS ctx0 x2"
 X_BUFS = 5
 ORDER_BUFS = 2
-ORDER_FROM = 9
+ORDER_FROM = 2
 WQ_AT = {3: 1, 5: 2, 7: 3}
 HEAD = "kb4 T0 kb2 T1 kb2 G0a G0bv qz0 G1a G1bv qz1 K0 gains K1 keepg tab qtab"
 
@@ -56,11 +56,16 @@ def body(text):
     return out
 
 
-BODY = body("L@3 K0 K1 T0@1 V0 T1@1 sqK0 sqK1 rK0 G0a@1 rK1 G0b@1 stK0 stK1 qz0@1 cV0 G1a@1 G1b@1 qz1@1 roK sK tab@1 Q V1 sqQ rQ stQ cV1 sV roQ sQ")
-FIRST_BODY = body("L@3 V0 sqK0 sqK1 rK0 rK1 stK0 stK1 T0@1 cV0 V1 G0a@1 G0b@1 T1@1 qz0@1 cV1 sV G1a@1 G1b@1 qz1@1 roK sK tab@1 Q sqQ rQ stQ roQ sQ")
-PRE_BODY = body("L@3 K0 K1 T0@1 V0 T1@1 sqK0 sqK1 rK0 G0a@1 rK1 G0b@1 stK0 stK1 qz0@1 cV0 sV0 G1a@1 G1b@1 qz1@1 roK sK tab@1 Q sqQ rQ stQ roQ")
-PRE2_BODY = body("L@3 K0 K1 T0@1 V0 T1@1 sqK0 sqK1 rK0 G0a@1 rK1 G0b@1 stK0 stK1 qz0@1 cV0 G1a@1 G1b@1 qz1@1 roK sK tab@1 Q V1 sqQ rQ stQ cV1 sV roQ sQ")
-LAST_BODY = body("Q sqQ rQ stQ roQ K0 K1 sqK0 rK0 stK0 sqK1 rK1 stK1 roK0 roK1 V1@-1 cV1@-1 V0 V1 cV0 cV1 sQ@-1 sV1@-1 sQ sV0 sK0 sV1 sK1")
+BODIES = [body(text) for text in [
+    "L@3 V0 sqK0 sqK1 rK0 rK1 stK0 stK1 T0@1 cV0 V1 G0a@1 G0b@1 T1@1 qz0@1 cV1 sV G1a@1 G1b@1 qz1@1 roK sK tab@1 Q sqQ rQ stQ roQ sQ",
+    "L@3 L@4 K0 K1 T0@1 V0 T1@1 sqK0 sqK1 rK0 G0a@1 rK1 G0b@1 stK0 stK1 qz0@1 cV0 G1a@1 G1b@1 qz1@1 roK sK tab@1 Q T0@2 V1 sqQ rQ stQ G0a@2 G0b@2 qz0@2 cV1 sV roQ sQ",
+    "L@4 K0 K1 T1@1 V0 T0@2 sqK0 sqK1 rK0 G1a@1 rK1 G1b@1 stK0 stK1 qz1@1 cV0 G0a@2 G0b@2 qz0@2 roK sK tab@1 Q T1@2 V1 sqQ rQ stQ G1a@2 G1b@2 qz1@2 cV1 sV roQ sQ",
+    "L@4 K0 K1 T0@2 V0 T1@2 sqK0 sqK1 rK0 G0a@2 rK1 G0b@2 stK0 stK1 qz0@2 cV0 G1a@2 G1b@2 qz1@2 roK sK tab@1 Q V1 sqQ rQ stQ cV1 sV roQ sQ",
+    "L@4 K0 K1 T0@2 V0 T1@2 sqK0 sqK1 rK0 G0a@2 rK1 G0b@2 stK0 stK1 qz0@2 cV0 G1a@2 G1b@2 qz1@2 roK sK tab@1 Q V1 sqQ rQ stQ cV1 sV roQ sQ",
+    "L@4 K0 K1 T0@2 V0 T1@2 sqK0 sqK1 rK0 G0a@2 rK1 G0b@2 stK0 stK1 qz0@2 cV0 sV0 G1a@2 G1b@2 qz1@2 roK sK tab@1 Q sqQ rQ stQ roQ sQ",
+    "K0 K1 Q V1@-1 sqK0 sqK1 rK0 rK1 stK0 stK1 sqQ cV1@-1 sV1@-1 rQ stQ tab@1 roQ roK sK",
+    "Q K0 K1 V0@-1 V1@-1 sqQ rQ sqK0 stQ roQ rK0 sqK1 sQ@-1 stK0 rK1 stK1 cV0@-1 sV0@-1 cV1@-1 sV1@-1 roK0 roK1 V0 V1 sQ sK0 sK1 cV0 sV0 cV1 sV1",
+]]
 FLOPS = 2 * HID * BATCH * ((CTX + Q_LEN) * 2 * KV_HEADS * HEAD_DIM + Q_LEN * Q_HEADS * HEAD_DIM)
 
 
@@ -511,13 +516,9 @@ def tile_dflashattention_pa_kernel(
             else:
                 step(s, 0)
         for n in range(len(rounds)):
-            for item in (FIRST_BODY if n == 0 else LAST_BODY if n == last_round else PRE_BODY if n == last_round - 1 else PRE2_BODY if n == last_round - 2 else BODY):
+            for item in BODIES[n]:
                 name, shift = item
                 m = n + shift
                 if m < 0 or m >= len(rounds):
-                    continue
-                if name[0] == "o" and m < ORDER_FROM:
-                    continue
-                if n > last_round and shift >= 0:
                     continue
                 step(name, m)

@@ -45,7 +45,7 @@ X_BUFS = 5
 ORDER_BUFS = 2
 ORDER_FROM = 2
 WQ_AT = {3: 1, 5: 2, 7: 3}
-HEAD = "kb4 T0 kb2 T1 kb2 G0a G0bv qz0 G1a G1bv qz1 K0 gains K1 keepg tab qtab"
+HEAD = "kb4 T0 kb3 T1 kb3 G0a G0bv qz0 G1a G1bv qz1 K0 gains K1 keepg tab qtab"
 
 
 def body(text):
@@ -57,14 +57,14 @@ def body(text):
 
 
 BODIES = [body(text) for text in [
-    "L@3 V0 sqK0 sqK1 rK0 rK1 stK0 stK1 T0@1 cV0 V1 G0a@1 G0b@1 T1@1 qz0@1 cV1 sV G1a@1 G1b@1 qz1@1 roK sK tab@1 Q sqQ rQ stQ roQ sQ",
-    "L@3 L@4 K0 K1 T0@1 V0 T1@1 sqK0 sqK1 rK0 G0a@1 rK1 G0b@1 stK0 stK1 qz0@1 cV0 G1a@1 G1b@1 qz1@1 roK sK tab@1 Q T0@2 V1 sqQ rQ stQ G0a@2 G0b@2 qz0@2 cV1 sV roQ sQ",
-    "L@4 K0 K1 T1@1 V0 T0@2 sqK0 sqK1 rK0 G1a@1 rK1 G1b@1 stK0 stK1 qz1@1 cV0 G0a@2 G0b@2 qz0@2 roK sK tab@1 Q T1@2 V1 sqQ rQ stQ G1a@2 G1b@2 qz1@2 cV1 sV roQ sQ",
-    "L@4 K0 K1 T0@2 V0 T1@2 sqK0 sqK1 rK0 G0a@2 rK1 G0b@2 stK0 stK1 qz0@2 cV0 G1a@2 G1b@2 qz1@2 roK sK tab@1 Q V1 sqQ rQ stQ cV1 sV roQ sQ",
-    "L@4 K0 K1 T0@2 V0 T1@2 sqK0 sqK1 rK0 G0a@2 rK1 G0b@2 stK0 stK1 qz0@2 cV0 G1a@2 G1b@2 qz1@2 roK sK tab@1 Q V1 sqQ rQ stQ cV1 sV roQ sQ",
-    "L@4 K0 K1 T0@2 V0 T1@2 sqK0 sqK1 rK0 G0a@2 rK1 G0b@2 stK0 stK1 qz0@2 cV0 sV0 G1a@2 G1b@2 qz1@2 roK sK tab@1 Q sqQ rQ stQ roQ sQ",
-    "K0 K1 Q V1@-1 sqK0 sqK1 rK0 rK1 stK0 stK1 sqQ cV1@-1 sV1@-1 rQ stQ tab@1 roQ roK sK",
-    "Q K0 K1 V0@-1 V1@-1 sqQ rQ sqK0 stQ roQ rK0 sqK1 sQ@-1 stK0 rK1 stK1 cV0@-1 sV0@-1 cV1@-1 sV1@-1 roK0 roK1 V0 V1 sQ sK0 sK1 cV0 sV0 cV1 sV1",
+    "L@3 V0 sqK0 rK0 sqK1 rK1 stK0 stK1 T0@1 cV0 V1 G0a@1 G0b@1 T1@1 qz0@1 cV1 sV G1a@1 G1b@1 qz1@1 roK sK tab@1 Q sqQ rQ stQ roQ sQ",
+    "L@3 L@4 K0 K1 T0@1 V0 T1@1 sqK0 rK0 sqK1 G0a@1 rK1 G0b@1 stK0 stK1 qz0@1 cV0 G1a@1 G1b@1 qz1@1 roK sK tab@1 Q T0@2 V1 sqQ rQ stQ G0a@2 G0b@2 qz0@2 cV1 sV roQ sQ",
+    "L@4 K0 K1 T1@1 V0 T0@2 sqK0 rK0 sqK1 G1a@1 rK1 G1b@1 stK0 stK1 qz1@1 cV0 G0a@2 G0b@2 qz0@2 roK sK tab@1 Q T1@2 V1 sqQ rQ stQ G1a@2 G1b@2 qz1@2 cV1 sV roQ sQ",
+    "L@4 K0 K1 T0@2 V0 T1@2 sqK0 rK0 sqK1 G0a@2 rK1 G0b@2 stK0 stK1 qz0@2 cV0 G1a@2 G1b@2 qz1@2 roK sK tab@1 Q V1 sqQ rQ stQ cV1 sV roQ sQ",
+    "L@4 K0 K1 T0@2 V0 T1@2 sqK0 rK0 sqK1 G0a@2 rK1 G0b@2 stK0 stK1 qz0@2 cV0 G1a@2 G1b@2 qz1@2 roK sK tab@1 Q V1 sqQ rQ stQ cV1 sV roQ sQ",
+    "L@4 K0 K1 T0@2 V0 T1@2 sqK0 rK0 sqK1 G0a@2 rK1 G0b@2 stK0 stK1 qz0@2 cV0 sV0 G1a@2 G1b@2 qz1@2 roK sK tab@1 Q sqQ rQ stQ roQ sQ",
+    "K0 K1 Q V1@-1 V0 sqK0 rK0 sqK1 rK1 stK0 stK1 sqQ cV1@-1 sV1@-1 rQ stQ tab@1 roQ cV0 sV0 roK sK",
+    "Q K0 K1 V1@-1 sqQ rQ sqK0 stQ roQ rK0 sqK1 sQ@-1 stK0 rK1 stK1 cV1@-1 sV1@-1 roK0 roK1 V0 VH cV0 cVH sQ sV0 sK0 sK1 sVHa sVHb",
 ]]
 FLOPS = 2 * HID * BATCH * ((CTX + Q_LEN) * 2 * KV_HEADS * HEAD_DIM + Q_LEN * Q_HEADS * HEAD_DIM)
 
@@ -484,6 +484,29 @@ def tile_dflashattention_pa_kernel(
                     t = done.tile([P, KV_HEADS, ROUND_SLOTS, HEAD_DIM], F32, name="values")
                     S["values"] = t
                 nc.scalar.copy(out=S["values"][:, :, j, :], in_=S["V%d" % j][:].rearrange("p (h d) -> p h d", h=KV_HEADS))
+            elif name == "VH":
+                S["V1"] = banks_pool.tile([P, UNIT_COLS], F32, name="bank")
+                for h in range(KV_HEADS):
+                    cols = slice(h * HEAD_DIM, (h + 1) * HEAD_DIM)
+                    for g in range(PASSES):
+                        tokens = slice(g * P, (g + 1) * P)
+                        nc.tensor.matmul_mx(
+                            out=S["V1"][:, cols],
+                            lhsT=x_codes[n][:, 1, tokens].bitcast(FP8X4),
+                            lhsT_scale=x_scales[n][:, 1, tokens],
+                            rhs=wv[0][:, g, 2 * h * HEAD_DIM : 2 * (h + 1) * HEAD_DIM].bitcast(FP4X4),
+                            rhs_scale=wv[1][:, g, cols],
+                            start=(g == 0),
+                            stop=(g == PASSES - 1),
+                        )
+            elif name == "cVH":
+                for h in range(KV_HEADS):
+                    nc.scalar.copy(out=S["values"][:, h, 1, :], in_=S["V1"][:, h * HEAD_DIM : (h + 1) * HEAD_DIM])
+            elif name in ("sVHa", "sVHb", "sVHc"):
+                hs = {"a": slice(0, 2), "b": slice(2, 4), "c": slice(3, 4)}[name[3]]
+                b, s = rounds[n][1]
+                rows = out_2[b, :, 0:CTX, :].rearrange("h (p i) d -> p h i d", i=CTX_SLOTS)[:, hs, s - 1, :]
+                nc.sync.dma_start(out=rows, in_=S["values"][:, hs, 1, :])
             elif name in ("sV", "sV0", "sV1"):
                 if name == "sV":
                     store_pair(S["values"][:], out_2, n)

@@ -60,8 +60,8 @@ BODIES = [body(text) for text in [
     "L@3 V0 sqK0 rK0 sqK1 rK1 stK0 stK1 T0@1 cV0 V1 G0a@1 G0b@1 T1@1 qz0@1 cV1 sV G1a@1 G1b@1 qz1@1 roK sK tab@1 Q sqQ rQ stQ roQ sQ",
     "L@3 L@4 K0 K1 T0@1 V0 T1@1 sqK0 rK0 sqK1 G0a@1 rK1 G0b@1 stK0 stK1 qz0@1 cV0 G1a@1 G1b@1 qz1@1 roK sK tab@1 Q T0@2 V1 sqQ rQ stQ G0a@2 G0b@2 qz0@2 cV1 sV roQ sQ",
     "L@4 K0 K1 T1@1 V0 T0@2 sqK0 rK0 sqK1 G1a@1 rK1 G1b@1 stK0 stK1 qz1@1 cV0 G0a@2 G0b@2 qz0@2 roK sK tab@1 Q T1@2 V1 sqQ rQ stQ G1a@2 G1b@2 qz1@2 cV1 sV roQ sQ",
-    "L@4 K0 K1 T0@2 V0 T1@2 sqK0 rK0 sqK1 G0a@2 rK1 G0b@2 stK0 stK1 qz0@2 cV0 G1a@2 G1b@2 qz1@2 roK sK tab@1 Q V1 sqQ rQ stQ cV1 sV roQ sQ",
-    "L@4 K0 K1 T0@2 V0 T1@2 sqK0 rK0 sqK1 G0a@2 rK1 G0b@2 stK0 stK1 qz0@2 cV0 G1a@2 G1b@2 qz1@2 roK sK tab@1 Q V1 sqQ rQ stQ cV1 sV roQ sQ",
+    "L@4 K0 K1 T0@2 V0 T1@2 sqK0 rK0 sqK1 G0a@2 rK1 G0b@2 stK0 stK1 qz0@2 o0@3 cV0 G1a@2 G1b@2 qz1@2 roK sK tab@1 Q V1 sqQ rQ stQ cV1 sV roQ sQ",
+    "L@4 K0 K1 T0@2 V0 T1@2 sqK0 rK0 sqK1 G0a@2 rK1 G0b@2 stK0 stK1 qz0@2 o0@3 cV0 G1a@2 G1b@2 qz1@2 roK sK tab@1 Q V1 sqQ rQ stQ cV1 sV roQ sQ",
     "L@4 K0 K1 T0@2 V0 T1@2 sqK0 rK0 sqK1 G0a@2 rK1 G0b@2 stK0 stK1 qz0@2 cV0 sV0 G1a@2 G1b@2 qz1@2 roK sK tab@1 Q sqQ rQ stQ roQ sQ",
     "K0 K1 Q V1@-1 V0 sqK0 rK0 sqK1 rK1 stK0 stK1 sqQ cV1@-1 sV1@-1 rQ stQ tab@1 roQ cV0 sV0 roK sK",
     "Q K0 K1 V1@-1 sqQ rQ sqK0 stQ roQ rK0 sqK1 sQ@-1 stK0 rK1 stK1 cV1@-1 sV1@-1 roK0 roK1 V0 VH cV0 cVH sQ sV0 sK0 sK1 sVHa sVHb",

from contextlib import ExitStack

import concourse.mybir as mybir
from concourse.masks import make_identity

F32 = mybir.dt.float32
BF16 = mybir.dt.bfloat16
I32 = mybir.dt.int32
U32 = mybir.dt.uint32
U8 = mybir.dt.uint8
FP8X4 = mybir.dt.float8_e4m3fn_x4
FP4X4 = mybir.dt.float4_e2m1fn_x4
ALU = mybir.AluOpType
ACT = mybir.ActivationFunctionType

P = 128
BATCH = 2
Q_LEN = 128
CTX = 896
HID = 2048
Q_HEADS = 16
KV_HEADS = 4
HEAD_DIM = 128
HALF = HEAD_DIM // 2
EPS = 1e-6

PACK = 4
K_PASS = P * PACK
PASSES = HID // K_PASS
PASS_WORDS = K_PASS // 2
UNIT_HEADS = 4
UNIT_COLS = UNIT_HEADS * HEAD_DIM
CTX_SLOTS = CTX // P
SLOTS = CTX_SLOTS + 1
ROUND_SLOTS = 2
ROUNDS = SLOTS // ROUND_SLOTS
assert ROUNDS == Q_HEADS // UNIT_HEADS
FIRST_PIECES = 2
ORDER_AHEAD = 2
LOADS_AHEAD = 3

WK_PARTS = 2
LOADS = "x0s0a x0s0b x0s1 wkS wkW gains wvW new wvS x1s0 x1s1 wqW wqS ctx0 x2"
X_BUFS = 5
ORDER_BUFS = 2
ORDER_FROM = 2
WQ_AT = {3: 1, 5: 2, 7: 3}
HEAD = "kb4 T0 kb3 T1 kb3 G0a G0bv qz0 G1a G1bv qz1 K0 gains K1 keepg tab qtab"


def body(text):
    out = []
    for w in text.split():
        parts = w.split("@")
        out.append((parts[0], int(parts[1]) if len(parts) == 2 else 0))
    return out


BODIES = [body(text) for text in [
    "L@3 V0 sqK0 rK0 sqK1 rK1 stK0 stK1 T0@1 cV0 V1 G0a@1 G0b@1 T1@1 qz0@1 cV1 sV G1a@1 G1b@1 qz1@1 roK sK tab@1 Q sqQ rQ stQ roQ sQ",
    "L@3 L@4 K0 K1 T0@1 V0 T1@1 sqK0 rK0 sqK1 G0a@1 rK1 G0b@1 stK0 stK1 qz0@1 cV0 G1a@1 G1b@1 qz1@1 roK sK tab@1 Q T0@2 V1 sqQ rQ stQ G0a@2 G0b@2 qz0@2 cV1 sV roQ sQ",
    "L@4 K0 K1 T1@1 V0 T0@2 sqK0 rK0 sqK1 G1a@1 rK1 G1b@1 stK0 stK1 qz1@1 cV0 G0a@2 G0b@2 qz0@2 roK sK tab@1 Q T1@2 V1 sqQ rQ stQ G1a@2 G1b@2 qz1@2 cV1 sV roQ sQ",
    "L@4 K0 K1 T0@2 V0 T1@2 sqK0 rK0 sqK1 G0a@2 rK1 G0b@2 stK0 stK1 qz0@2 o0@3 cV0 G1a@2 G1b@2 qz1@2 roK sK tab@1 Q V1 sqQ rQ stQ cV1 sV roQ sQ",
    "L@4 K0 K1 T0@2 V0 T1@2 sqK0 rK0 sqK1 G0a@2 rK1 G0b@2 stK0 stK1 qz0@2 o0@3 cV0 G1a@2 G1b@2 qz1@2 roK sK tab@1 Q V1 sqQ rQ stQ cV1 sV roQ sQ",
    "L@4 K0 K1 T0@2 V0 T1@2 sqK0 rK0 sqK1 G0a@2 rK1 G0b@2 stK0 stK1 qz0@2 cV0 sV0 G1a@2 G1b@2 qz1@2 roK sK tab@1 Q sqQ rQ stQ roQ sQ",
    "K0 K1 Q V1@-1 V0 sqK0 rK0 sqK1 rK1 stK0 stK1 sqQ cV1@-1 sV1@-1 rQ stQ tab@1 roQ cV0 sV0 roK sK",
    "Q K0 K1 V1@-1 sqQ rQ sqK0 stQ roQ rK0 sqK1 sQ@-1 stK0 rK1 stK1 cV1@-1 sV1@-1 roK0 roK1 V0 VH cV0 cVH sQ sV0 sK0 sK1 sVHa sVHb",
]]
FLOPS = 2 * HID * BATCH * ((CTX + Q_LEN) * 2 * KV_HEADS * HEAD_DIM + Q_LEN * Q_HEADS * HEAD_DIM)


def context_rows(rows):
    return rows.rearrange("(p i) w -> p i w", i=CTX_SLOTS)


def tile_dflashattention_pa_kernel(
    tc,
    hidden_states,
    target_hidden,
    cos,
    sin,
    Wq_words,
    Wq_scales,
    Wk_words,
    Wk_scales,
    Wv_words,
    Wv_scales,
    q_norm_w,
    k_norm_w,
    out_0,
    out_1,
    out_2,
):
    nc = tc.nc
    rounds = [((0, 0), (1, 0))]
    for b in range(BATCH):
        for s in range(1, CTX_SLOTS, ROUND_SLOTS):
            rounds.append(((b, s), (b, s + 1)))
        if b == 0:
            rounds.append(((0, CTX_SLOTS), (1, CTX_SLOTS)))
    last_round = len(rounds) - 1

    with ExitStack() as ctx:
        keep = ctx.enter_context(tc.tile_pool(name="keep", bufs=1))
        x_pool = ctx.enter_context(tc.tile_pool(name="x_pool", bufs=X_BUFS))
        order_pool = ctx.enter_context(tc.tile_pool(name="order_pool", bufs=ORDER_BUFS))
        table_pool = ctx.enter_context(tc.tile_pool(name="table_pool", bufs=3))
        stage = ctx.enter_context(tc.tile_pool(name="stage", bufs=3))
        small = ctx.enter_context(tc.tile_pool(name="small", bufs=4))
        scratch = ctx.enter_context(tc.tile_pool(name="scratch", bufs=2))
        work = ctx.enter_context(tc.tile_pool(name="work", bufs=2))
        done = ctx.enter_context(tc.tile_pool(name="done", bufs=3))
        banks_pool = ctx.enter_context(tc.psum_pool(name="banks_pool", bufs=8))
        ctx.enter_context(tc.manual_schedule())

        x_codes = []
        x_scales = []
        for n in range(len(rounds)):
            x_codes.append(keep.tile([P, ROUND_SLOTS, PASSES * P], U32, name="x_codes_%d" % n, align_bytes=64))
            x_scales.append(keep.tile([P, ROUND_SLOTS, PASSES * P], U8, name="x_scales_%d" % n, align_bytes=64))
        q_table = keep.tile([P, BATCH, 2, HEAD_DIM], F32, name="q_table")
        new_cos = keep.tile([P, BATCH, HEAD_DIM], BF16, name="new_cos")
        new_sin = keep.tile([P, BATCH, HEAD_DIM], BF16, name="new_sin")
        context_cos = [keep.tile([P, CTX_SLOTS, HEAD_DIM], BF16, name="context_cos_%d" % b) for b in range(BATCH)]
        context_sin = [keep.tile([P, CTX_SLOTS, HEAD_DIM], BF16, name="context_sin_%d" % b) for b in range(BATCH)]

        def weight_tiles(name):
            words_sb = keep.tile([P, PASSES, 2 * UNIT_COLS], U8, name=name + "_words", align_bytes=64)
            plane = keep.tile([P, PASSES, UNIT_COLS], U8, name=name + "_scales", align_bytes=64)
            return words_sb, plane

        wk = weight_tiles("wk")
        wv = weight_tiles("wv")
        wq = [weight_tiles("wq%d" % c) for c in range(4)]
        gain_rows = keep.tile([P, 2 * HEAD_DIM], BF16, name="gain_rows")
        ones = keep.tile([P, P], BF16, name="ones")
        gains = keep.tile([P, 2 * HEAD_DIM], F32, name="gains")
        signed_gains = keep.tile([P, 2, 2, HALF], F32, name="signed_gains")
        signed_rows = signed_gains[:].rearrange("p r s j -> p r (s j)")
        k_gain = (gains[:, 0:HEAD_DIM], signed_rows[:, 0, :])
        q_gain = (gains[:, HEAD_DIM : 2 * HEAD_DIM], signed_rows[:, 1, :])
        identity = keep.tile([P, P], F32, name="identity")
        eps = keep.tile([P, 1], F32, name="eps")
        table_warmer = keep.tile([P, 1], F32, name="table_warmer")
        idle_rows = keep.tile([P, UNIT_COLS], BF16, name="idle_rows")

        nc.vector.memset(ones[:], 1.0)
        nc.vector.memset(idle_rows[:], 0.0)
        nc.vector.memset(gain_rows[:], 0.0)
        nc.vector.memset(eps[:], EPS)
        for words_sb, plane in [wk, wv] + wq:
            nc.vector.memset(plane[:].bitcast(I32), 0)
        make_identity(nc, identity[:])
        nc.scalar.activation(out=table_warmer[:], in_=eps[:], func=ACT.Abs_reciprocal_sqrt)

        x_tiles = {}
        ordered_words = {}

        def load_x(n):
            x_tile = x_pool.tile([P, ROUND_SLOTS, HID], BF16, name="x")
            x_tiles[n] = x_tile
            if n == 0:
                width = HID // FIRST_PIECES
                for j in range(ROUND_SLOTS):
                    for i in range(FIRST_PIECES):
                        columns = slice(i * width, (i + 1) * width)
                        nc.sync.dma_start(out=x_tile[:, j, columns], in_=hidden_states[j, :, columns])
                return
            (b0, s0), (b1, s1) = rounds[n]
            if b0 == b1:
                nc.sync.dma_start(out=x_tile[:], in_=context_rows(target_hidden[b0])[:, s0 - 1 : s1, :])
            else:
                for j, (b, s) in enumerate(rounds[n]):
                    nc.sync.dma_start(out=x_tile[:, j, :], in_=context_rows(target_hidden[b])[:, s - 1, :])

        def load_weight(tiles, words, scales, first_column, parts=1):
            words_sb, plane = tiles
            first = first_column // 4
            for r in range(4):
                nc.sync.dma_start(
                    out=plane[r:P:32, :, :].bitcast(I32),
                    in_=scales.bitcast(I32)[:, r:16:4, first : first + UNIT_COLS // 4].rearrange("g q n -> q g n"),
                )
            first = first_column // 2
            for g in range(0, PASSES, PASSES // parts):
                gs = slice(g, g + PASSES // parts)
                nc.sync.dma_start(
                    out=words_sb[:, gs, :].bitcast(I32),
                    in_=words.bitcast(I32)[gs, :, first : first + UNIT_COLS // 2].rearrange("g p n -> p g n"),
                )

        def load_query_weight(c):
            load_weight(wq[c], Wq_words, Wq_scales, c * UNIT_COLS)

        def load_new_angles():
            for table_sb, table in ((new_cos, cos), (new_sin, sin)):
                nc.sync.dma_start(out=table_sb[:], in_=table[:, CTX : CTX + Q_LEN, :].rearrange("b p d -> p b d"))

        def load_context_angles(b):
            for table_sb, table in ((context_cos[b], cos), (context_sin[b], sin)):
                nc.sync.dma_start(out=table_sb[:], in_=context_rows(table[b, 0:CTX, :]))

        def load_ahead(n):
            if n < len(rounds):
                load_x(n)
            if n == 4:
                load_context_angles(1)
            if n in WQ_AT:
                load_query_weight(WQ_AT[n])

        for s in LOADS.split():
            if s[0] == "x":
                if len(s) == 2:
                    load_x(int(s[1]))
                else:
                    n, j = int(s[1]), int(s[3])
                    if n not in x_tiles:
                        t = x_pool.tile([P, ROUND_SLOTS, HID], BF16, name="x")
                        x_tiles[n] = t
                    b, sl = rounds[n][j]
                    cols = slice(0, HID) if len(s) == 4 else slice(1024 * "ab".index(s[4]), 1024 * "ab".index(s[4]) + 1024)
                    rows = hidden_states[j, :, :] if n == 0 else context_rows(target_hidden[b])[:, sl - 1, :]
                    nc.sync.dma_start(out=x_tiles[n][:, j, cols], in_=rows[:, cols])
            elif s == "gains":
                nc.sync.dma_start(out=gain_rows[0:1, 0:HEAD_DIM], in_=k_norm_w.unsqueeze(0))
                nc.sync.dma_start(out=gain_rows[0:1, HEAD_DIM : 2 * HEAD_DIM], in_=q_norm_w.unsqueeze(0))
            elif s == "wk":
                load_weight(wk, Wk_words, Wk_scales, 0, WK_PARTS)
            elif s == "wkS":
                for r in range(4):
                    nc.sync.dma_start(
                        out=wk[1][r:P:32, :, :].bitcast(I32),
                        in_=Wk_scales.bitcast(I32)[:, r:16:4, :].rearrange("g q n -> q g n"),
                    )
            elif s[:3] == "wkW":
                gs = slice(0, 4) if len(s) == 3 else slice(2 * int(s[3]), 2 * int(s[3]) + 2)
                nc.sync.dma_start(out=wk[0][:, gs, :].bitcast(I32), in_=Wk_words.bitcast(I32)[gs, :, :].rearrange("g p n -> p g n"))
            elif s == "wv":
                load_weight(wv, Wv_words, Wv_scales, 0)
            elif s == "wvS":
                for r in range(4):
                    nc.sync.dma_start(
                        out=wv[1][r:P:32, :, :].bitcast(I32),
                        in_=Wv_scales.bitcast(I32)[:, r:16:4, :].rearrange("g q n -> q g n"),
                    )
            elif s == "wvW":
                nc.sync.dma_start(out=wv[0][:].bitcast(I32), in_=Wv_words.bitcast(I32).rearrange("g p n -> p g n"))
            elif s == "wqW":
                nc.sync.dma_start(out=wq[0][0][:].bitcast(I32), in_=Wq_words.bitcast(I32)[:, :, 0:256].rearrange("g p n -> p g n"))
            elif s == "wqS":
                for r in range(4):
                    nc.sync.dma_start(
                        out=wq[0][1][r:P:32, :, :].bitcast(I32),
                        in_=Wq_scales.bitcast(I32)[:, r:16:4, 0:128].rearrange("g q n -> q g n"),
                    )
            elif s == "new":
                load_new_angles()
            elif s == "ctx0":
                load_context_angles(0)
            elif s == "ctx1":
                load_context_angles(1)
            elif s == "wq":
                load_query_weight(0)
            else:
                raise ValueError(s)

        def spread_gains():
            bank = banks_pool.tile([P, UNIT_COLS], F32, name="bank")
            nc.tensor.matmul(out=bank[:, 0 : 2 * HEAD_DIM], lhsT=ones[:], rhs=gain_rows[:], start=True, stop=True)
            return bank

        def keep_gains(bank):
            nc.scalar.copy(out=gains[:], in_=bank[:, 0 : 2 * HEAD_DIM])
            halves = bank[:, 0 : 2 * HEAD_DIM].rearrange("p (r s j) -> p r s j", r=2, s=2)
            nc.scalar.copy(out=signed_gains[:, :, 0, :], in_=halves[:, :, 0, :])
            nc.scalar.mul(out=signed_gains[:, :, 1, :], in_=halves[:, :, 1, :], mul=-1.0)

        def make_table(table, cos_rows, sin_rows, gain):
            count = table.shape[1]
            gain, signed_gain = gain

            def spread(columns):
                return columns.unsqueeze(1).to_broadcast([P, count, HEAD_DIM])

            nc.gpsimd.tensor_tensor(out=table[:, :, 0, :], in0=cos_rows, in1=spread(gain), op=ALU.mult)
            halves = "p r (s j) -> p r s j"
            nc.gpsimd.tensor_tensor(
                out=table[:, :, 1, :].rearrange(halves, s=2),
                in0=sin_rows.rearrange(halves, s=2)[:, :, ::-1, :],
                in1=spread(signed_gain).rearrange(halves, s=2),
                op=ALU.mult,
            )

        k_tables = {}

        def make_key_table(n):
            table = table_pool.tile([P, ROUND_SLOTS, 2, HEAD_DIM], F32, name="k_table")
            k_tables[n] = table
            if n == 0:
                make_table(table[:], new_cos[:], new_sin[:], k_gain)
                return
            (b0, s0), (b1, s1) = rounds[n]
            if b0 == b1:
                slots = slice(s0 - 1, s1)
                make_table(table[:], context_cos[b0][:, slots, :], context_sin[b0][:, slots, :], k_gain)
            else:
                for j, (b, s) in enumerate(rounds[n]):
                    slots = slice(s - 1, s)
                    make_table(table[:, j : j + 1], context_cos[b][:, slots, :], context_sin[b][:, slots, :], k_gain)

        def order_words(n, j, copy):
            ordered = order_pool.tile([P, HID // 2], F32, name="ordered")
            ordered_words[(n, j)] = ordered
            copy(
                out=ordered[:].rearrange("p (g u r) -> p g r u", g=PASSES, u=2),
                in_=x_tiles[n][:, j, :].bitcast(F32).rearrange("p (g r u) -> p g r u", g=PASSES, u=2),
            )

        t_banks = {}

        def transpose_slot(n, j):
            t_banks[(n, j)] = []
            for first_pass in range(0, PASSES, 2):
                bank = banks_pool.tile([P, 2, 2, P], F32, name="bank")
                for i in range(2):
                    start = (first_pass + i) * PASS_WORDS
                    for u in range(2):
                        if (n, j) in ordered_words:
                            words = ordered_words[(n, j)][:, start + u * P : start + (u + 1) * P]
                        else:
                            words = x_tiles[n][:, j, :].bitcast(F32)[:, start + u : start + PASS_WORDS : 2]
                        nc.tensor.transpose(bank[:, i, u, :], words, identity[:])
                t_banks[(n, j)].append(bank)

        grouped = {}

        def group(n, j, half, copy):
            if half == 0:
                g = stage.tile([P, PASSES * P * PACK], BF16, name="grouped", align_bytes=64)
                grouped[(n, j)] = g
            words = grouped[(n, j)][:].bitcast(F32).rearrange("p (g r u) -> p g r u", g=PASSES, u=2)
            copy(
                out=words[:, 2 * half : 2 * half + 2, :, :],
                in_=t_banks[(n, j)][half][:].rearrange("p g u r -> p g r u"),
            )

        def quantise(n, j):
            nc.vector.quantize_mx(
                out=x_codes[n][:, j, :].bitcast(FP8X4), scales=x_scales[n][:, j, :], in_=grouped[(n, j)][:]
            )

        def project(n, j, weight):
            words_sb, plane = weight
            acc = banks_pool.tile([P, UNIT_COLS], F32, name="bank")
            for g in range(PASSES):
                tokens = slice(g * P, (g + 1) * P)
                nc.tensor.matmul_mx(
                    out=acc[:],
                    lhsT=x_codes[n][:, j, tokens].bitcast(FP8X4),
                    lhsT_scale=x_scales[n][:, j, tokens],
                    rhs=words_sb[:, g, :].bitcast(FP4X4),
                    rhs_scale=plane[:, g, :],
                    start=(g == 0),
                    stop=(g == PASSES - 1),
                )
            return acc

        def squares(acc, sum_squares, first):
            unread = scratch.tile([P, UNIT_HEADS, HEAD_DIM], F32, name="squares")
            for h in range(UNIT_HEADS):
                nc.scalar.activation(
                    out=unread[:, h, :],
                    in_=acc[:, h * HEAD_DIM : (h + 1) * HEAD_DIM],
                    func=ACT.Square,
                    accum_out=sum_squares[:, first + h : first + h + 1],
                )

        def rsqrt(out, sums):
            nc.scalar.activation(out=out, in_=sums, func=ACT.Abs_reciprocal_sqrt, scale=1.0 / HEAD_DIM, bias=eps[:])

        def norm_and_scale(acc, inv_rms, table, products):
            for h in range(UNIT_HEADS):
                head = acc[:, h * HEAD_DIM : (h + 1) * HEAD_DIM]
                nc.vector.scalar_tensor_tensor(
                    out=products[:, h, :, :],
                    in0=head.unsqueeze(1).to_broadcast([P, 2, HEAD_DIM]),
                    scalar=inv_rms[:, h : h + 1],
                    in1=table,
                    op0=ALU.mult,
                    op1=ALU.mult,
                )

        def rotate(products, result, adder):
            halves = "p r (s j) -> p r s j"
            adder.tensor_tensor(
                out=result.rearrange(halves, s=2),
                in0=products[:, :, 0, :].rearrange(halves, s=2),
                in1=products[:, :, 1, :].rearrange(halves, s=2)[:, :, ::-1, :],
                op=ALU.add,
            )

        def store_slot(tile, out, n, j):
            b, s = rounds[n][j]
            if s == 0:
                rows = out[b, :, CTX : CTX + Q_LEN, :].rearrange("h p d -> p h d")
            else:
                rows = out[b, :, 0:CTX, :].rearrange("h (p i) d -> p h i d", i=CTX_SLOTS)[:, :, s - 1, :]
            nc.sync.dma_start(out=rows, in_=tile[:, :, j, :])

        def store_pair(tile, out, n):
            (b0, s0), (b1, s1) = rounds[n]
            if b0 != b1 :
                for j in range(ROUND_SLOTS):
                    store_slot(tile, out, n, j)
            else:
                context = out[b0, :, 0:CTX, :].rearrange("h (p i) d -> p h i d", i=CTX_SLOTS)
                nc.sync.dma_start(out=context[:, :, s0 - 1 : s1, :], in_=tile)

        st = {}

        def step(name, n):
            S = st.setdefault(n, {})
            if name in ("K0", "K1"):
                S[name] = project(n, int(name[1]), wk)
            elif name in ("V0", "V1"):
                S[name] = project(n, int(name[1]), wv)
            elif name == "Q":
                S["Q"] = project(0, n % 2, wq[n // 2])
            elif name in ("T0", "T1"):
                transpose_slot(n, int(name[1]))
            elif name[0] == "G":
                group(n, int(name[1]), "ab".index(name[2]), nc.vector.tensor_copy if name[3:] == "v" else nc.scalar.copy)
            elif name in ("qz0", "qz1"):
                quantise(n, int(name[2]))
            elif name in ("sqK0", "sqK1"):
                if "ssK" not in S:
                    t = small.tile([P, 8], F32, name="sum_squares")
                    u = small.tile([P, 8], F32, name="inv_rms")
                    S["ssK"] = t
                    S["inK"] = u
                squares(S[name[2:]], S["ssK"], 4 * int(name[3]))
            elif name in ("rK", "rK0", "rK1"):
                c = slice(0, 8) if name == "rK" else slice(4 * int(name[2]), 4 * int(name[2]) + 4)
                rsqrt(S["inK"][:, c], S["ssK"][:, c])
            elif name == "sqQ":
                t = small.tile([P, 4], F32, name="sum_squares_q")
                u = small.tile([P, 4], F32, name="inv_rms_q")
                S["ssQ"] = t
                S["inQ"] = u
                squares(S["Q"], t, 0)
            elif name == "rQ":
                rsqrt(S["inQ"][:], S["ssQ"][:])
            elif name in ("stK0", "stK1"):
                j = int(name[3])
                if "pK" not in S:
                    t = work.tile([P, KV_HEADS * ROUND_SLOTS, 2, HEAD_DIM], F32, name="k_products")
                    u = done.tile([P, KV_HEADS * ROUND_SLOTS, HEAD_DIM], F32, name="keys")
                    S["pK"] = t
                    S["keys"] = u
                norm_and_scale(S["K%d" % j], S["inK"][:, 4 * j : 4 * j + 4], k_tables[n][:, j, :, :], S["pK"][:, j : 8 : 2, :, :])
            elif name in ("roK", "roKg", "roK0", "roK1", "roK0g", "roK1g"):
                r = slice(0, 8) if name in ("roK", "roKg") else slice(int(name[3]), 8, 2)
                rotate(S["pK"][:, r], S["keys"][:, r], nc.gpsimd if name[-1] == "g" else nc.vector)
            elif name in ("sK", "sK0", "sK1"):
                pair = S["keys"][:].rearrange("p (h i) d -> p h i d", i=ROUND_SLOTS)
                if name == "sK":
                    store_pair(pair, out_1, n)
                else:
                    store_slot(pair, out_1, n, int(name[2]))
            elif name == "stQ":
                t = work.tile([P, UNIT_HEADS, 2, HEAD_DIM], F32, name="q_products")
                u = done.tile([P, UNIT_HEADS, HEAD_DIM], F32, name="queries")
                S["pQ"] = t
                S["queries"] = u
                norm_and_scale(S["Q"], S["inQ"], q_table[:, n % 2, :, :], t)
            elif name in ("roQ", "roQv"):
                rotate(S["pQ"], S["queries"][:], nc.vector if name == "roQv" else nc.gpsimd)
            elif name == "sQ":
                heads = slice((n // 2) * UNIT_HEADS, (n // 2 + 1) * UNIT_HEADS)
                nc.sync.dma_start(out=out_0[n % 2, heads, :, :].rearrange("h p d -> p h d"), in_=S["queries"][:])
            elif name in ("cV0", "cV1"):
                j = int(name[2])
                if "values" not in S:
                    t = done.tile([P, KV_HEADS, ROUND_SLOTS, HEAD_DIM], F32, name="values")
                    S["values"] = t
                nc.scalar.copy(out=S["values"][:, :, j, :], in_=S["V%d" % j][:].rearrange("p (h d) -> p h d", h=KV_HEADS))
            elif name == "VH":
                S["V1"] = banks_pool.tile([P, UNIT_COLS], F32, name="bank")
                for h in range(KV_HEADS):
                    cols = slice(h * HEAD_DIM, (h + 1) * HEAD_DIM)
                    for g in range(PASSES):
                        tokens = slice(g * P, (g + 1) * P)
                        nc.tensor.matmul_mx(
                            out=S["V1"][:, cols],
                            lhsT=x_codes[n][:, 1, tokens].bitcast(FP8X4),
                            lhsT_scale=x_scales[n][:, 1, tokens],
                            rhs=wv[0][:, g, 2 * h * HEAD_DIM : 2 * (h + 1) * HEAD_DIM].bitcast(FP4X4),
                            rhs_scale=wv[1][:, g, cols],
                            start=(g == 0),
                            stop=(g == PASSES - 1),
                        )
            elif name == "cVH":
                for h in range(KV_HEADS):
                    nc.scalar.copy(out=S["values"][:, h, 1, :], in_=S["V1"][:, h * HEAD_DIM : (h + 1) * HEAD_DIM])
            elif name in ("sVHa", "sVHb", "sVHc"):
                hs = {"a": slice(0, 2), "b": slice(2, 4), "c": slice(3, 4)}[name[3]]
                b, s = rounds[n][1]
                rows = out_2[b, :, 0:CTX, :].rearrange("h (p i) d -> p h i d", i=CTX_SLOTS)[:, hs, s - 1, :]
                nc.sync.dma_start(out=rows, in_=S["values"][:, hs, 1, :])
            elif name in ("sV", "sV0", "sV1"):
                if name == "sV":
                    store_pair(S["values"][:], out_2, n)
                else:
                    store_slot(S["values"][:], out_2, n, int(name[2]))
            elif name == "tab":
                make_key_table(n)
            elif name in ("o0", "o1", "o0s", "o1s"):
                order_words(n, int(name[1]), nc.scalar.copy if name[2:] == "s" else nc.vector.tensor_copy)
            elif name == "L":
                load_ahead(n)
            else:
                raise ValueError(name)

        idle_bank = banks_pool.tile([P, UNIT_COLS], F32, name="bank")

        def keep_busy(count):
            for i in range(count):
                nc.tensor.matmul(out=idle_bank[:], lhsT=ones[:], rhs=idle_rows[:], start=True, stop=True)

        for s in HEAD.split():
            if s == "gains":
                gains_bank = spread_gains()
            elif s == "keepg":
                keep_gains(gains_bank)
            elif s == "qtab":
                make_table(q_table[:], new_cos[:], new_sin[:], q_gain)
            elif s[:2] == "kb":
                keep_busy(int(s[2:]))
            else:
                step(s, 0)
        for n in range(len(rounds)):
            for item in BODIES[n]:
                name, shift = item
                m = n + shift
                if m < 0 or m >= len(rounds):
                    continue
                step(name, m)
